import numpy as np
import ml_dtypes


def mxq(x, axis, fmt="e4m3"):
    dtype, down = {"e4m3": (ml_dtypes.float8_e4m3fn, 7), "e5m2": (ml_dtypes.float8_e5m2, 14)}[fmt]
    v = np.moveaxis(np.asarray(x, np.float32).astype(ml_dtypes.bfloat16).astype(np.float64), axis, -1)
    blocks = v.reshape(v.shape[:-1] + (-1, 32))
    amax = np.abs(blocks).max(-1, keepdims=True)
    byte = np.maximum(np.where(amax > 0, np.frexp(amax)[1] - 1 + 127, 0) - down, 1)
    scale = np.exp2(byte - 127.0)
    codes = (blocks / scale).astype(np.float32).astype(dtype).astype(np.float64)
    return np.moveaxis((codes * scale).reshape(v.shape), -1, axis)


WIDE = False


def mx_kscale(k):
    if not WIDE:
        return np.ones(k)
    levels = np.array([10, -10, 5, -5, 0])
    a = np.random.permutation(np.resize(levels, k // 512 * 4)).reshape(k // 512, 4)
    idx = np.arange(k)
    return np.exp2(a[idx // 512, idx % 128 // 32])


BF16 = ml_dtypes.bfloat16


def bf(x):
    return np.asarray(x, np.float32).astype(BF16)


def f64(x):
    return np.asarray(x).astype(np.float64)


B, NV, S, D, H = 2, 8, 128, 1024, 8
HD = D // H


def setup_inputs():
    s, t = mx_kscale(D), mx_kscale(D)
    return {"x": bf(np.random.standard_normal((B * NV, S, D)) * s),
            "scores": bf(np.random.standard_normal((B, NV, NV, H, S)) * 1.4),
            "Wv": bf(np.random.standard_normal((D, D)) / np.sqrt(D) / s[:, None] * t),
            "bv": bf(np.random.standard_normal(D) * 0.3 * t),
            "Wo": bf(np.random.standard_normal((D, D)) / np.sqrt(D) / t[:, None]),
            "bo": bf(np.random.standard_normal(D) * 0.3)}


def reference(x, scores, Wv, bv, Wo, bo):
    v = (mxq(f64(x), 2, "e4m3") @ mxq(f64(Wv), 0, "e4m3")) + f64(bv)
    v = v.reshape(B, NV, S, H, HD).transpose(0, 1, 3, 2, 4)
    sc = f64(scores)
    e = np.exp(sc - sc.max(2, keepdims=True))
    w = e / e.sum(2, keepdims=True)
    mixed = np.zeros((B, NV, H, S, HD))
    for j in range(NV):
        mixed = mixed + w[:, :, j, :, :, None] * v[:, j][:, None]
    mixed = mixed.transpose(0, 1, 3, 2, 4).reshape(B * NV, S, D)
    return (mxq(mixed, 2, "e4m3") @ mxq(f64(Wo), 0, "e4m3")) + f64(bo)

@@ -1,0 +1,337 @@
+from contextlib import ExitStack
+
+import concourse.mybir as mybir
+from concourse.masks import make_identity
+
+F32 = mybir.dt.float32
+BF16 = mybir.dt.bfloat16
+U32 = mybir.dt.uint32
+U8 = mybir.dt.uint8
+FP8X4 = mybir.dt.float8_e4m3fn_x4
+ADD = mybir.AluOpType.add
+SUBTRACT = mybir.AluOpType.subtract
+MULT = mybir.AluOpType.mult
+MAX = mybir.AluOpType.max
+INNERMOST = mybir.AxisListType.X
+EXP = mybir.ActivationFunctionType.Exp
+
+P = 128
+SCENES, VIEWS, POSITIONS, FEATURES, HEADS = 2, 8, 128, 1024, 8
+PACK = 4
+K_PASS = P * PACK
+PASSES = FEATURES // K_PASS
+N_TILE = 512
+N_HALVES = FEATURES // N_TILE
+GROUP_POS = P // VIEWS
+CHUNKS = POSITIONS // GROUP_POS
+GROUPS = SCENES * CHUNKS
+
+PIECE_CHUNKS = 2
+PIECE_GROUPS = PIECE_CHUNKS * SCENES
+PIECE_POS = PIECE_CHUNKS * GROUP_POS
+PIECES = CHUNKS // PIECE_CHUNKS
+
+AHEAD_V = 2
+AHEAD_X = 2
+AHEAD_W = 2
+BEHIND_Y = 2
+
+FLOPS = 2 * 2 * SCENES * VIEWS * POSITIONS * FEATURES * FEATURES + 2 * SCENES * VIEWS * VIEWS * POSITIONS * FEATURES
+
+
+def tile_crossviewattention_pa_kernel(tc, x, scores, Wv, bv, Wo, bo, out):
+    nc = tc.nc
+    with ExitStack() as ctx:
+        keep = ctx.enter_context(tc.tile_pool(name="keep", bufs=1))
+        x_stage = ctx.enter_context(tc.tile_pool(name="x_stage", bufs=3))
+        w_stage = ctx.enter_context(tc.tile_pool(name="w_stage", bufs=4))
+        v_pool = ctx.enter_context(tc.tile_pool(name="v_pool", bufs=AHEAD_V + 2))
+        s_pool = ctx.enter_context(tc.tile_pool(name="s_pool", bufs=2))
+        mixw_pool = ctx.enter_context(tc.tile_pool(name="mixw_pool", bufs=4))
+        m_pool = ctx.enter_context(tc.tile_pool(name="m_pool", bufs=BEHIND_Y + 2))
+        y_pool = ctx.enter_context(tc.tile_pool(name="y_pool", bufs=6))
+        psum = ctx.enter_context(tc.psum_pool(name="psum", bufs=2))
+
+        def chunk_and_scene(grp):
+            return divmod(grp, SCENES)
+
+        def group_rows(dram, grp, cols):
+            c, b = chunk_and_scene(grp)
+            block = dram[b * VIEWS : (b + 1) * VIEWS, c * GROUP_POS : (c + 1) * GROUP_POS, cols]
+            return block.rearrange("j s k -> s j k")
+
+        x_raw = keep.tile([P, GROUPS, FEATURES], BF16)
+        x_codes = keep.tile([P, GROUPS, PASSES * P], U32, align_bytes=64)
+        x_scales = keep.tile([P, GROUPS, PASSES * P], U8, align_bytes=64)
+        wv_raw = keep.tile([P, PASSES, PACK, FEATURES], BF16)
+        wv_codes = keep.tile([P, PASSES, FEATURES], U32, align_bytes=64)
+        wv_scales = keep.tile([P, PASSES, FEATURES], U8, align_bytes=64)
+        wo_raw = keep.tile([P, PASSES, PACK, FEATURES], BF16)
+        wo_codes = keep.tile([P, PASSES, FEATURES], U32, align_bytes=64)
+        wo_scales = keep.tile([P, PASSES, FEATURES], U8, align_bytes=64)
+        score_raw = keep.tile([P, VIEWS, POSITIONS], BF16)
+        bv_rows = keep.tile([P, P], BF16)
+        bo_all = keep.tile([P, FEATURES], BF16)
+
+        def load_tokens(grp):
+            nc.sync.dma_start(out=x_raw[:, grp, :], in_=group_rows(x, grp, slice(0, FEATURES)))
+
+        def load_wv(g):
+            nc.sync.dma_start(
+                out=wv_raw[:, g, :, :].rearrange("p (u e) n -> p u (e n)", e=2),
+                in_=Wv[g * K_PASS : (g + 1) * K_PASS, :].rearrange("(u p e) n -> p u (e n)", u=2, e=2),
+            )
+
+        def load_scores(j):
+            nc.scalar.dma_start(
+                out=score_raw[:, j, :], in_=scores[:, :, j, :, :].rearrange("b i h s -> (b i) h s")
+            )
+
+        nc.vector.memset(bv_rows[:], 0.0)
+        for j in range(VIEWS - 2):
+            load_scores(j)
+        load_tokens(0)
+        load_wv(0)
+        for j in range(VIEWS - 2, VIEWS):
+            load_scores(j)
+        load_wv(1)
+        nc.scalar.dma_start(out=bv_rows[0:HEADS, :], in_=bv.rearrange("(h c) -> h c", c=P))
+        for grp in range(1, 6):
+            load_tokens(grp)
+        for g in range(PASSES):
+            nc.sync.dma_start(
+                out=wo_raw[:, g, :, :],
+                in_=Wo[g * K_PASS : (g + 1) * K_PASS, :].rearrange("(t p) n -> p t n", p=P),
+            )
+        for grp in range(6, GROUPS):
+            load_tokens(grp)
+        nc.sync.dma_start(out=bo_all[:], in_=bo.partition_broadcast(P))
+
+        ident = keep.tile([P, P], F32)
+        make_identity(nc, ident[:])
+        same_pos = keep.tile([P, GROUP_POS], F32)
+        nc.vector.tensor_reduce(
+            out=same_pos[:], in_=ident[:].rearrange("p (s i) -> p s i", i=VIEWS), axis=INNERMOST, op=ADD
+        )
+        block_mask = keep.tile([P, GROUP_POS, VIEWS], F32)
+        nc.vector.tensor_copy(
+            out=block_mask[:], in_=same_pos[:].unsqueeze(2).to_broadcast([P, GROUP_POS, VIEWS])
+        )
+
+        def regroup_weights(copy, raw, g, half):
+            cols = slice(half * N_TILE, (half + 1) * N_TILE)
+            grouped_w = w_stage.tile([P, N_TILE, PACK], BF16, align_bytes=64)
+            copy(
+                out=grouped_w[:].rearrange("p (c i) t -> p c t i", i=4),
+                in_=raw[:, g, :, cols].rearrange("p t (c i) -> p c t i", i=4),
+            )
+            return grouped_w
+
+        def quantise_weights(grouped_w, codes, scales, g, half):
+            cols = slice(half * N_TILE, (half + 1) * N_TILE)
+            nc.vector.quantize_mx(
+                out=codes[:, g, cols].bitcast(FP8X4),
+                scales=scales[:, g, cols],
+                in_=grouped_w[:].rearrange("p n t -> p (n t)"),
+            )
+
+        def prepare_weights(raw, codes, scales, g):
+            first = regroup_weights(nc.vector.tensor_copy, raw, g, 0)
+            second = regroup_weights(nc.scalar.copy, raw, g, 1)
+            quantise_weights(first, codes, scales, g, 0)
+            quantise_weights(second, codes, scales, g, 1)
+
+        grouped_tokens = {}
+
+        def transpose_tokens(grp):
+            words = x_raw[:, grp, :].bitcast(F32)
+            flipped = psum.tile([P, PACK, P], F32, tag="flip")
+            for c in range(PACK):
+                nc.tensor.transpose(flipped[:, c, :], words[:, c * P : (c + 1) * P], ident[:])
+            grouped_x = x_stage.tile([P, PASSES, P, PACK], BF16, align_bytes=64)
+            nc.scalar.copy(
+                out=grouped_x[:].bitcast(F32), in_=flipped[:].rearrange("p (g u) n -> p g n u", u=2)
+            )
+            grouped_tokens[grp] = grouped_x
+
+        def quantise_tokens(grp):
+            nc.vector.quantize_mx(
+                out=x_codes[:, grp, :].bitcast(FP8X4),
+                scales=x_scales[:, grp, :],
+                in_=grouped_tokens[grp][:].rearrange("p g n t -> p (g n t)"),
+            )
+
+        weights_t = keep.tile([P, CHUNKS, SCENES, HEADS, VIEWS], F32)
+
+        def softmax_piece(piece):
+            shape = [P, PIECE_POS, VIEWS]
+            by_pos = score_raw[:, :, piece * PIECE_POS : (piece + 1) * PIECE_POS].rearrange("p j s -> p s j")
+            top = s_pool.tile([P, PIECE_POS], F32)
+            nc.vector.tensor_reduce(out=top[:], in_=by_pos, axis=INNERMOST, op=MAX)
+            expd = s_pool.tile(shape, F32)
+            nc.vector.tensor_tensor(out=expd[:], in0=by_pos, in1=top[:].unsqueeze(2).to_broadcast(shape), op=SUBTRACT)
+            nc.scalar.activation(out=expd[:], in_=expd[:], func=EXP)
+            total = s_pool.tile([P, PIECE_POS], F32)
+            nc.vector.tensor_reduce(out=total[:], in_=expd[:], axis=INNERMOST, op=ADD)
+            inverse = s_pool.tile([P, PIECE_POS], F32)
+            nc.vector.reciprocal(out=inverse[:], in_=total[:])
+            weights = s_pool.tile([P, PIECE_CHUNKS, P], F32)
+            nc.vector.tensor_tensor(
+                out=weights[:].rearrange("p c (s j) -> p (c s) j", j=VIEWS),
+                in0=expd[:],
+                in1=inverse[:].unsqueeze(2).to_broadcast(shape),
+                op=MULT,
+            )
+            flipped = psum.tile([P, PACK, P], F32, tag="flip")
+            for c in range(PIECE_CHUNKS):
+                nc.tensor.transpose(flipped[:, c, :], weights[:, c, :], ident[:])
+            chunks = slice(piece * PIECE_CHUNKS, (piece + 1) * PIECE_CHUNKS)
+            nc.scalar.copy(
+                out=weights_t[:, chunks].rearrange("p c b h i -> p (c b) h i"),
+                in_=flipped[:, 0:PIECE_CHUNKS, :].rearrange("p c (b i h) -> p (c b) h i", b=SCENES, i=VIEWS),
+            )
+
+        def bias_columns():
+            bv_wide = keep.tile([P, P], F32)
+            nc.vector.tensor_copy(out=bv_wide[:], in_=bv_rows[:])
+            flipped = psum.tile([P, PACK, P], F32, tag="flip")
+            nc.tensor.transpose(flipped[:, 0, :], bv_wide[:], ident[:])
+            bv_cols = keep.tile([P, HEADS], F32)
+            nc.vector.tensor_copy(out=bv_cols[:], in_=flipped[:, 0, 0:HEADS])
+            return bv_cols
+
+        values = {}
+        mix_weights = {}
+        mix_sums = {}
+        mixed_tokens = {}
+        mixed_codes = {}
+        out_sums = {}
+
+        def first_projection(grp):
+            v_rows = v_pool.tile([P, FEATURES], F32)
+            for half in range(N_HALVES):
+                cols = slice(half * N_TILE, (half + 1) * N_TILE)
+                acc = psum.tile([P, N_TILE], F32, tag="acc_v")
+                for g in range(PASSES):
+                    toks = slice(g * P, (g + 1) * P)
+                    nc.tensor.matmul_mx(
+                        out=acc[:],
+                        lhsT=x_codes[:, grp, toks].bitcast(FP8X4),
+                        lhsT_scale=x_scales[:, grp, toks],
+                        rhs=wv_codes[:, g, cols].bitcast(FP8X4),
+                        rhs_scale=wv_scales[:, g, cols],
+                        start=(g == 0),
+                        stop=(g == PASSES - 1),
+                    )
+                nc.scalar.copy(out=v_rows[:, cols], in_=acc[:])
+            values[grp] = v_rows
+
+        def build_mix_weights(grp):
+            c, b = chunk_and_scene(grp)
+            shape = [P, HEADS, GROUP_POS, VIEWS]
+            mixw = mixw_pool.tile(shape, F32)
+            nc.gpsimd.tensor_tensor(
+                out=mixw[:],
+                in0=weights_t[:, c, b, :, :].unsqueeze(2).to_broadcast(shape),
+                in1=block_mask[:].unsqueeze(1).to_broadcast(shape),
+                op=MULT,
+            )
+            mix_weights[grp] = mixw
+
+        def mix(grp):
+            sums = []
+            for g in range(PASSES):
+                acc = psum.tile([P, PACK, P], F32, tag="acc_mix")
+                for t in range(PACK):
+                    h = g * PACK + t
+                    nc.tensor.matmul(
+                        out=acc[:, t, :],
+                        lhsT=values[grp][:, h * P : (h + 1) * P],
+                        rhs=mix_weights[grp][:, h, :, :].rearrange("p s i -> p (s i)"),
+                        start=True,
+                        stop=True,
+                    )
+                sums.append(acc)
+            mix_sums[grp] = sums
+
+        def round_mixed(grp, bv_cols):
+            mixed = m_pool.tile([P, PASSES, P, PACK], BF16, align_bytes=64)
+            for g in range(PASSES):
+                nc.vector.tensor_tensor(
+                    out=mixed[:, g, :, :],
+                    in0=mix_sums[grp][g][:].rearrange("p t n -> p n t"),
+                    in1=bv_cols[:, g * PACK : (g + 1) * PACK].unsqueeze(1).to_broadcast([P, P, PACK]),
+                    op=ADD,
+                )
+            mixed_tokens[grp] = mixed
+
+        def quantise_mixed(grp):
+            m_codes = m_pool.tile([P, PASSES * P], U32, align_bytes=64)
+            m_scales = m_pool.tile([P, PASSES * P], U8, align_bytes=64)
+            nc.vector.quantize_mx(
+                out=m_codes[:].bitcast(FP8X4),
+                scales=m_scales[:],
+                in_=mixed_tokens[grp][:].rearrange("p g n t -> p (g n t)"),
+            )
+            mixed_codes[grp] = (m_codes, m_scales)
+
+        def second_projection(grp):
+            m_codes, m_scales = mixed_codes[grp]
+            sums = []
+            for half in range(N_HALVES):
+                cols = slice(half * N_TILE, (half + 1) * N_TILE)
+                acc = psum.tile([P, N_TILE], F32, tag="acc_y")
+                for g in range(PASSES):
+                    toks = slice(g * P, (g + 1) * P)
+                    nc.tensor.matmul_mx(
+                        out=acc[:],
+                        lhsT=m_codes[:, toks].bitcast(FP8X4),
+                        lhsT_scale=m_scales[:, toks],
+                        rhs=wo_codes[:, g, cols].bitcast(FP8X4),
+                        rhs_scale=wo_scales[:, g, cols],
+                        start=(g == 0),
+                        stop=(g == PASSES - 1),
+                    )
+                sums.append(acc)
+            out_sums[grp] = sums
+
+        def finish(grp):
+            for half in range(N_HALVES):
+                cols = slice(half * N_TILE, (half + 1) * N_TILE)
+                result = y_pool.tile([P, N_TILE], F32)
+                nc.vector.tensor_tensor(out=result[:], in0=out_sums[grp][half][:], in1=bo_all[:, cols], op=ADD)
+                nc.sync.dma_start(out=group_rows(out, grp, cols), in_=result[:])
+
+        def is_group(grp):
+            return 0 <= grp < GROUPS
+
+        first_step = -(AHEAD_V + AHEAD_X)
+        bv_cols = None
+        for step in range(first_step, GROUPS + BEHIND_Y):
+            if is_group(step - 1):
+                round_mixed(step - 1, bv_cols)
+            if is_group(step - BEHIND_Y):
+                second_projection(step - BEHIND_Y)
+                finish(step - BEHIND_Y)
+            if is_group(step - 1):
+                quantise_mixed(step - 1)
+            if is_group(step + AHEAD_V):
+                first_projection(step + AHEAD_V)
+            if is_group(step + AHEAD_V + AHEAD_X):
+                transpose_tokens(step + AHEAD_V + AHEAD_X)
+            if is_group(step + AHEAD_V + AHEAD_X - 1):
+                quantise_tokens(step + AHEAD_V + AHEAD_X - 1)
+            if step == first_step:
+                for g in range(PASSES):
+                    prepare_weights(wv_raw, wv_codes, wv_scales, g)
+            piece, offset = divmod(step + PIECE_GROUPS, PIECE_GROUPS)
+            if offset == 0 and 0 <= piece < PIECES:
+                softmax_piece(piece)
+            if 0 <= step + PASSES < PASSES:
+                prepare_weights(wo_raw, wo_codes, wo_scales, step + PASSES)
+            if step == -1:
+                bv_cols = bias_columns()
+            if is_group(step + AHEAD_W):
+                build_mix_weights(step + AHEAD_W)
+            if is_group(step):
+                mix(step)

@@ -35,6 +35,7 @@ AHEAD_V = 2
 AHEAD_X = 2
 AHEAD_W = 2
 BEHIND_Y = 2
+FIRST_STEP = -(AHEAD_W + 3)
 
 FLOPS = 2 * 2 * SCENES * VIEWS * POSITIONS * FEATURES * FEATURES + 2 * SCENES * VIEWS * VIEWS * POSITIONS * FEATURES
 
@@ -45,12 +46,13 @@ def tile_crossviewattention_pa_kernel(tc, x, scores, Wv, bv, Wo, bo, out):
         keep = ctx.enter_context(tc.tile_pool(name="keep", bufs=1))
         x_stage = ctx.enter_context(tc.tile_pool(name="x_stage", bufs=3))
         w_stage = ctx.enter_context(tc.tile_pool(name="w_stage", bufs=4))
-        v_pool = ctx.enter_context(tc.tile_pool(name="v_pool", bufs=AHEAD_V + 2))
         s_pool = ctx.enter_context(tc.tile_pool(name="s_pool", bufs=2))
-        mixw_pool = ctx.enter_context(tc.tile_pool(name="mixw_pool", bufs=4))
+        v_pool = ctx.enter_context(tc.tile_pool(name="v_pool", bufs=AHEAD_V + 2))
+        mixw_pool = ctx.enter_context(tc.tile_pool(name="mixw_pool", bufs=AHEAD_W + 2))
         m_pool = ctx.enter_context(tc.tile_pool(name="m_pool", bufs=BEHIND_Y + 2))
         y_pool = ctx.enter_context(tc.tile_pool(name="y_pool", bufs=6))
         psum = ctx.enter_context(tc.psum_pool(name="psum", bufs=2))
+        ctx.enter_context(tc.manual_schedule())
 
         def chunk_and_scene(grp):
             return divmod(grp, SCENES)
@@ -59,6 +61,9 @@ def tile_crossviewattention_pa_kernel(tc, x, scores, Wv, bv, Wo, bo, out):
             c, b = chunk_and_scene(grp)
             block = dram[b * VIEWS : (b + 1) * VIEWS, c * GROUP_POS : (c + 1) * GROUP_POS, cols]
             return block.rearrange("j s k -> s j k")
+
+        def half_cols(half):
+            return slice(half * N_TILE, (half + 1) * N_TILE)
 
         x_raw = keep.tile([P, GROUPS, FEATURES], BF16)
         x_codes = keep.tile([P, GROUPS, PASSES * P], U32, align_bytes=64)
@@ -82,6 +87,12 @@ def tile_crossviewattention_pa_kernel(tc, x, scores, Wv, bv, Wo, bo, out):
                 in_=Wv[g * K_PASS : (g + 1) * K_PASS, :].rearrange("(u p e) n -> p u (e n)", u=2, e=2),
             )
 
+        def load_wo(g):
+            nc.sync.dma_start(
+                out=wo_raw[:, g, :, :],
+                in_=Wo[g * K_PASS : (g + 1) * K_PASS, :].rearrange("(t p) n -> p t n", p=P),
+            )
+
         def load_scores(j):
             nc.scalar.dma_start(
                 out=score_raw[:, j, :], in_=scores[:, :, j, :, :].rearrange("b i h s -> (b i) h s")
@@ -96,14 +107,11 @@ def tile_crossviewattention_pa_kernel(tc, x, scores, Wv, bv, Wo, bo, out):
             load_scores(j)
         load_wv(1)
         nc.scalar.dma_start(out=bv_rows[0:HEADS, :], in_=bv.rearrange("(h c) -> h c", c=P))
-        for grp in range(1, 6):
+        for grp in range(1, AHEAD_V + AHEAD_X):
             load_tokens(grp)
         for g in range(PASSES):
-            nc.sync.dma_start(
-                out=wo_raw[:, g, :, :],
-                in_=Wo[g * K_PASS : (g + 1) * K_PASS, :].rearrange("(t p) n -> p t n", p=P),
-            )
-        for grp in range(6, GROUPS):
+            load_wo(g)
+        for grp in range(AHEAD_V + AHEAD_X, GROUPS):
             load_tokens(grp)
         nc.sync.dma_start(out=bo_all[:], in_=bo.partition_broadcast(P))
 
@@ -118,28 +126,24 @@ def tile_crossviewattention_pa_kernel(tc, x, scores, Wv, bv, Wo, bo, out):
             out=block_mask[:], in_=same_pos[:].unsqueeze(2).to_broadcast([P, GROUP_POS, VIEWS])
         )
 
-        def regroup_weights(copy, raw, g, half):
-            cols = slice(half * N_TILE, (half + 1) * N_TILE)
-            grouped_w = w_stage.tile([P, N_TILE, PACK], BF16, align_bytes=64)
-            copy(
-                out=grouped_w[:].rearrange("p (c i) t -> p c t i", i=4),
-                in_=raw[:, g, :, cols].rearrange("p t (c i) -> p c t i", i=4),
-            )
-            return grouped_w
+        grouped_weights = {}
 
-        def quantise_weights(grouped_w, codes, scales, g, half):
-            cols = slice(half * N_TILE, (half + 1) * N_TILE)
-            nc.vector.quantize_mx(
-                out=codes[:, g, cols].bitcast(FP8X4),
-                scales=scales[:, g, cols],
-                in_=grouped_w[:].rearrange("p n t -> p (n t)"),
-            )
+        def regroup_weights(name, raw, g):
+            for half, copy in enumerate((nc.vector.tensor_copy, nc.scalar.copy)):
+                grouped_w = w_stage.tile([P, N_TILE, PACK], BF16, align_bytes=64)
+                copy(
+                    out=grouped_w[:].rearrange("p (c i) t -> p c t i", i=4),
+                    in_=raw[:, g, :, half_cols(half)].rearrange("p t (c i) -> p c t i", i=4),
+                )
+                grouped_weights[(name, g, half)] = grouped_w
 
-        def prepare_weights(raw, codes, scales, g):
-            first = regroup_weights(nc.vector.tensor_copy, raw, g, 0)
-            second = regroup_weights(nc.scalar.copy, raw, g, 1)
-            quantise_weights(first, codes, scales, g, 0)
-            quantise_weights(second, codes, scales, g, 1)
+        def quantise_weights(name, codes, scales, g):
+            for half in range(N_HALVES):
+                nc.vector.quantize_mx(
+                    out=codes[:, g, half_cols(half)].bitcast(FP8X4),
+                    scales=scales[:, g, half_cols(half)],
+                    in_=grouped_weights[(name, g, half)][:].rearrange("p n t -> p (n t)"),
+                )
 
         grouped_tokens = {}
 
@@ -162,43 +166,59 @@ def tile_crossviewattention_pa_kernel(tc, x, scores, Wv, bv, Wo, bo, out):
             )
 
         weights_t = keep.tile([P, CHUNKS, SCENES, HEADS, VIEWS], F32)
+        piece_shape = [P, PIECE_POS, VIEWS]
+        exponents = {}
+        piece_weights = {}
 
-        def softmax_piece(piece):
-            shape = [P, PIECE_POS, VIEWS]
+        def softmax_shift(piece):
             by_pos = score_raw[:, :, piece * PIECE_POS : (piece + 1) * PIECE_POS].rearrange("p j s -> p s j")
             top = s_pool.tile([P, PIECE_POS], F32)
             nc.vector.tensor_reduce(out=top[:], in_=by_pos, axis=INNERMOST, op=MAX)
-            expd = s_pool.tile(shape, F32)
-            nc.vector.tensor_tensor(out=expd[:], in0=by_pos, in1=top[:].unsqueeze(2).to_broadcast(shape), op=SUBTRACT)
-            nc.scalar.activation(out=expd[:], in_=expd[:], func=EXP)
+            expd = s_pool.tile(piece_shape, F32)
+            nc.vector.tensor_tensor(
+                out=expd[:], in0=by_pos, in1=top[:].unsqueeze(2).to_broadcast(piece_shape), op=SUBTRACT
+            )
+            exponents[piece] = expd
+
+        def softmax_exp(piece):
+            nc.scalar.activation(out=exponents[piece][:], in_=exponents[piece][:], func=EXP)
+
+        def softmax_normalise(piece):
             total = s_pool.tile([P, PIECE_POS], F32)
-            nc.vector.tensor_reduce(out=total[:], in_=expd[:], axis=INNERMOST, op=ADD)
+            nc.vector.tensor_reduce(out=total[:], in_=exponents[piece][:], axis=INNERMOST, op=ADD)
             inverse = s_pool.tile([P, PIECE_POS], F32)
             nc.vector.reciprocal(out=inverse[:], in_=total[:])
             weights = s_pool.tile([P, PIECE_CHUNKS, P], F32)
             nc.vector.tensor_tensor(
                 out=weights[:].rearrange("p c (s j) -> p (c s) j", j=VIEWS),
-                in0=expd[:],
-                in1=inverse[:].unsqueeze(2).to_broadcast(shape),
+                in0=exponents[piece][:],
+                in1=inverse[:].unsqueeze(2).to_broadcast(piece_shape),
                 op=MULT,
             )
+            piece_weights[piece] = weights
+
+        def softmax_transpose(piece):
             flipped = psum.tile([P, PACK, P], F32, tag="flip")
             for c in range(PIECE_CHUNKS):
-                nc.tensor.transpose(flipped[:, c, :], weights[:, c, :], ident[:])
+                nc.tensor.transpose(flipped[:, c, :], piece_weights[piece][:, c, :], ident[:])
             chunks = slice(piece * PIECE_CHUNKS, (piece + 1) * PIECE_CHUNKS)
             nc.scalar.copy(
                 out=weights_t[:, chunks].rearrange("p c b h i -> p (c b) h i"),
                 in_=flipped[:, 0:PIECE_CHUNKS, :].rearrange("p c (b i h) -> p (c b) h i", b=SCENES, i=VIEWS),
             )
 
+        def piece_that_starts_at(grp):
+            piece, offset = divmod(grp, PIECE_GROUPS)
+            return piece if offset == 0 and 0 <= piece < PIECES else None
+
+        bv_cols = keep.tile([P, HEADS], F32)
+
         def bias_columns():
             bv_wide = keep.tile([P, P], F32)
             nc.vector.tensor_copy(out=bv_wide[:], in_=bv_rows[:])
             flipped = psum.tile([P, PACK, P], F32, tag="flip")
             nc.tensor.transpose(flipped[:, 0, :], bv_wide[:], ident[:])
-            bv_cols = keep.tile([P, HEADS], F32)
             nc.vector.tensor_copy(out=bv_cols[:], in_=flipped[:, 0, 0:HEADS])
-            return bv_cols
 
         values = {}
         mix_weights = {}
@@ -210,7 +230,6 @@ def tile_crossviewattention_pa_kernel(tc, x, scores, Wv, bv, Wo, bo, out):
         def first_projection(grp):
             v_rows = v_pool.tile([P, FEATURES], F32)
             for half in range(N_HALVES):
-                cols = slice(half * N_TILE, (half + 1) * N_TILE)
                 acc = psum.tile([P, N_TILE], F32, tag="acc_v")
                 for g in range(PASSES):
                     toks = slice(g * P, (g + 1) * P)
@@ -218,12 +237,12 @@ def tile_crossviewattention_pa_kernel(tc, x, scores, Wv, bv, Wo, bo, out):
                         out=acc[:],
                         lhsT=x_codes[:, grp, toks].bitcast(FP8X4),
                         lhsT_scale=x_scales[:, grp, toks],
-                        rhs=wv_codes[:, g, cols].bitcast(FP8X4),
-                        rhs_scale=wv_scales[:, g, cols],
+                        rhs=wv_codes[:, g, half_cols(half)].bitcast(FP8X4),
+                        rhs_scale=wv_scales[:, g, half_cols(half)],
                         start=(g == 0),
                         stop=(g == PASSES - 1),
                     )
-                nc.scalar.copy(out=v_rows[:, cols], in_=acc[:])
+                nc.scalar.copy(out=v_rows[:, half_cols(half)], in_=acc[:])
             values[grp] = v_rows
 
         def build_mix_weights(grp):
@@ -254,7 +273,7 @@ def tile_crossviewattention_pa_kernel(tc, x, scores, Wv, bv, Wo, bo, out):
                 sums.append(acc)
             mix_sums[grp] = sums
 
-        def round_mixed(grp, bv_cols):
+        def round_mixed(grp):
             mixed = m_pool.tile([P, PASSES, P, PACK], BF16, align_bytes=64)
             for g in range(PASSES):
                 nc.vector.tensor_tensor(
@@ -279,7 +298,6 @@ def tile_crossviewattention_pa_kernel(tc, x, scores, Wv, bv, Wo, bo, out):
             m_codes, m_scales = mixed_codes[grp]
             sums = []
             for half in range(N_HALVES):
-                cols = slice(half * N_TILE, (half + 1) * N_TILE)
                 acc = psum.tile([P, N_TILE], F32, tag="acc_y")
                 for g in range(PASSES):
                     toks = slice(g * P, (g + 1) * P)
@@ -287,8 +305,8 @@ def tile_crossviewattention_pa_kernel(tc, x, scores, Wv, bv, Wo, bo, out):
                         out=acc[:],
                         lhsT=m_codes[:, toks].bitcast(FP8X4),
                         lhsT_scale=m_scales[:, toks],
-                        rhs=wo_codes[:, g, cols].bitcast(FP8X4),
-                        rhs_scale=wo_scales[:, g, cols],
+                        rhs=wo_codes[:, g, half_cols(half)].bitcast(FP8X4),
+                        rhs_scale=wo_scales[:, g, half_cols(half)],
                         start=(g == 0),
                         stop=(g == PASSES - 1),
                     )
@@ -297,40 +315,60 @@ def tile_crossviewattention_pa_kernel(tc, x, scores, Wv, bv, Wo, bo, out):
 
         def finish(grp):
             for half in range(N_HALVES):
-                cols = slice(half * N_TILE, (half + 1) * N_TILE)
                 result = y_pool.tile([P, N_TILE], F32)
-                nc.vector.tensor_tensor(out=result[:], in0=out_sums[grp][half][:], in1=bo_all[:, cols], op=ADD)
-                nc.sync.dma_start(out=group_rows(out, grp, cols), in_=result[:])
+                nc.vector.tensor_tensor(
+                    out=result[:], in0=out_sums[grp][half][:], in1=bo_all[:, half_cols(half)], op=ADD
+                )
+                nc.sync.dma_start(out=group_rows(out, grp, half_cols(half)), in_=result[:])
 
         def is_group(grp):
             return 0 <= grp < GROUPS
 
-        first_step = -(AHEAD_V + AHEAD_X)
-        bv_cols = None
-        for step in range(first_step, GROUPS + BEHIND_Y):
+        def is_pass(g):
+            return 0 <= g < PASSES
+
+        wv_start = -(AHEAD_V + AHEAD_X)
+        wo_start = BEHIND_Y - PASSES - 1
+        for step in range(FIRST_STEP, GROUPS + BEHIND_Y):
             if is_group(step - 1):
-                round_mixed(step - 1, bv_cols)
+                round_mixed(step - 1)
             if is_group(step - BEHIND_Y):
                 second_projection(step - BEHIND_Y)
                 finish(step - BEHIND_Y)
             if is_group(step - 1):
                 quantise_mixed(step - 1)
+            if is_pass(step - wv_start - 1):
+                quantise_weights("wv", wv_codes, wv_scales, step - wv_start - 1)
+            if is_pass(step - wo_start - 1):
+                quantise_weights("wo", wo_codes, wo_scales, step - wo_start - 1)
             if is_group(step + AHEAD_V):
                 first_projection(step + AHEAD_V)
+
+            piece = piece_that_starts_at(step + AHEAD_W + 2)
+            if piece is not None:
+                softmax_exp(piece)
+            if is_pass(step - wv_start):
+                regroup_weights("wv", wv_raw, step - wv_start)
+            if is_pass(step - wo_start):
+                regroup_weights("wo", wo_raw, step - wo_start)
+
             if is_group(step + AHEAD_V + AHEAD_X):
                 transpose_tokens(step + AHEAD_V + AHEAD_X)
+            piece = piece_that_starts_at(step + AHEAD_W + 1)
+            if piece is not None:
+                softmax_transpose(piece)
             if is_group(step + AHEAD_V + AHEAD_X - 1):
                 quantise_tokens(step + AHEAD_V + AHEAD_X - 1)
-            if step == first_step:
-                for g in range(PASSES):
-                    prepare_weights(wv_raw, wv_codes, wv_scales, g)
-            piece, offset = divmod(step + PIECE_GROUPS, PIECE_GROUPS)
-            if offset == 0 and 0 <= piece < PIECES:
-                softmax_piece(piece)
-            if 0 <= step + PASSES < PASSES:
-                prepare_weights(wo_raw, wo_codes, wo_scales, step + PASSES)
-            if step == -1:
-                bv_cols = bias_columns()
+            if step == -AHEAD_V:
+                bias_columns()
+
+            piece = piece_that_starts_at(step + AHEAD_W + 2)
+            if piece is not None:
+                softmax_normalise(piece)
+            piece = piece_that_starts_at(step + AHEAD_W + 3)
+            if piece is not None:
+                softmax_shift(piece)
+
             if is_group(step + AHEAD_W):
                 build_mix_weights(step + AHEAD_W)
             if is_group(step):

@@ -21,21 +21,21 @@ PACK = 4
 K_PASS = P * PACK
 PASSES = FEATURES // K_PASS
 N_TILE = 512
-N_HALVES = FEATURES // N_TILE
+HALVES = FEATURES // N_TILE
 GROUP_POS = P // VIEWS
 CHUNKS = POSITIONS // GROUP_POS
-GROUPS = SCENES * CHUNKS
+UNITS = HALVES * CHUNKS
 
 PIECE_CHUNKS = 2
-PIECE_GROUPS = PIECE_CHUNKS * SCENES
 PIECE_POS = PIECE_CHUNKS * GROUP_POS
 PIECES = CHUNKS // PIECE_CHUNKS
 
-AHEAD_V = 2
+AHEAD_V = 1
 AHEAD_X = 2
-AHEAD_W = 2
+AHEAD_W = 1
 BEHIND_Y = 2
 FIRST_STEP = -(AHEAD_W + 3)
+LAST_STEP = UNITS + BEHIND_Y - 1
 
 FLOPS = 2 * 2 * SCENES * VIEWS * POSITIONS * FEATURES * FEATURES + 2 * SCENES * VIEWS * VIEWS * POSITIONS * FEATURES
 
@@ -49,37 +49,40 @@ def tile_crossviewattention_pa_kernel(tc, x, scores, Wv, bv, Wo, bo, out):
         s_pool = ctx.enter_context(tc.tile_pool(name="s_pool", bufs=2))
         v_pool = ctx.enter_context(tc.tile_pool(name="v_pool", bufs=AHEAD_V + 2))
         mixw_pool = ctx.enter_context(tc.tile_pool(name="mixw_pool", bufs=AHEAD_W + 2))
-        m_pool = ctx.enter_context(tc.tile_pool(name="m_pool", bufs=BEHIND_Y + 2))
-        y_pool = ctx.enter_context(tc.tile_pool(name="y_pool", bufs=6))
-        psum = ctx.enter_context(tc.psum_pool(name="psum", bufs=2))
+        m_pool = ctx.enter_context(tc.tile_pool(name="m_pool", bufs=3))
+        y_pool = ctx.enter_context(tc.tile_pool(name="y_pool", bufs=8))
+        psum = ctx.enter_context(tc.psum_pool(name="psum", bufs=8))
         ctx.enter_context(tc.manual_schedule())
 
-        def chunk_and_scene(grp):
-            return divmod(grp, SCENES)
-
-        def group_rows(dram, grp, cols):
-            c, b = chunk_and_scene(grp)
-            block = dram[b * VIEWS : (b + 1) * VIEWS, c * GROUP_POS : (c + 1) * GROUP_POS, cols]
+        def group_rows(dram, chunk, b, cols):
+            block = dram[b * VIEWS : (b + 1) * VIEWS, chunk * GROUP_POS : (chunk + 1) * GROUP_POS, cols]
             return block.rearrange("j s k -> s j k")
 
         def half_cols(half):
             return slice(half * N_TILE, (half + 1) * N_TILE)
 
-        x_raw = keep.tile([P, GROUPS, FEATURES], BF16)
-        x_codes = keep.tile([P, GROUPS, PASSES * P], U32, align_bytes=64)
-        x_scales = keep.tile([P, GROUPS, PASSES * P], U8, align_bytes=64)
+        def tokens(index):
+            return slice(index * P, (index + 1) * P)
+
+        x_raw = keep.tile([P, CHUNKS, SCENES, FEATURES], BF16)
+        x_codes = keep.tile([P, CHUNKS, SCENES * PASSES * P], U32, align_bytes=64)
+        x_scales = keep.tile([P, CHUNKS, SCENES * PASSES * P], U8, align_bytes=64)
+        m_codes = keep.tile([P, PASSES, CHUNKS, SCENES * P], U32, align_bytes=64)
+        m_scales = keep.tile([P, PASSES, CHUNKS, SCENES * P], U8, align_bytes=64)
         wv_raw = keep.tile([P, PASSES, PACK, FEATURES], BF16)
         wv_codes = keep.tile([P, PASSES, FEATURES], U32, align_bytes=64)
         wv_scales = keep.tile([P, PASSES, FEATURES], U8, align_bytes=64)
         wo_raw = keep.tile([P, PASSES, PACK, FEATURES], BF16)
         wo_codes = keep.tile([P, PASSES, FEATURES], U32, align_bytes=64)
         wo_scales = keep.tile([P, PASSES, FEATURES], U8, align_bytes=64)
+        wv_tiles = {"name": "wv", "raw": wv_raw, "codes": wv_codes, "scales": wv_scales}
+        wo_tiles = {"name": "wo", "raw": wo_raw, "codes": wo_codes, "scales": wo_scales}
         score_raw = keep.tile([P, VIEWS, POSITIONS], BF16)
         bv_rows = keep.tile([P, P], BF16)
         bo_all = keep.tile([P, FEATURES], BF16)
 
-        def load_tokens(grp):
-            nc.sync.dma_start(out=x_raw[:, grp, :], in_=group_rows(x, grp, slice(0, FEATURES)))
+        def load_tokens(chunk, b):
+            nc.sync.dma_start(out=x_raw[:, chunk, b, :], in_=group_rows(x, chunk, b, slice(0, FEATURES)))
 
         def load_wv(g):
             nc.sync.dma_start(
@@ -95,24 +98,24 @@ def tile_crossviewattention_pa_kernel(tc, x, scores, Wv, bv, Wo, bo, out):
 
         def load_scores(j):
             nc.scalar.dma_start(
-                out=score_raw[:, j, :], in_=scores[:, :, j, :, :].rearrange("b i h s -> (b i) h s")
+                out=score_raw[:, j, :], in_=scores[:, :, j, :, :].rearrange("b i h s -> h (b i) s")
             )
 
         nc.vector.memset(bv_rows[:], 0.0)
         for j in range(VIEWS - 2):
             load_scores(j)
-        load_tokens(0)
+        load_tokens(0, 0)
         load_wv(0)
         for j in range(VIEWS - 2, VIEWS):
             load_scores(j)
+        load_tokens(0, 1)
         load_wv(1)
         nc.scalar.dma_start(out=bv_rows[0:HEADS, :], in_=bv.rearrange("(h c) -> h c", c=P))
-        for grp in range(1, AHEAD_V + AHEAD_X):
-            load_tokens(grp)
+        for chunk in range(1, CHUNKS):
+            for b in range(SCENES):
+                load_tokens(chunk, b)
         for g in range(PASSES):
             load_wo(g)
-        for grp in range(AHEAD_V + AHEAD_X, GROUPS):
-            load_tokens(grp)
         nc.sync.dma_start(out=bo_all[:], in_=bo.partition_broadcast(P))
 
         ident = keep.tile([P, P], F32)
@@ -128,44 +131,43 @@ def tile_crossviewattention_pa_kernel(tc, x, scores, Wv, bv, Wo, bo, out):
 
         grouped_weights = {}
 
-        def regroup_weights(name, raw, g):
-            for half, copy in enumerate((nc.vector.tensor_copy, nc.scalar.copy)):
-                grouped_w = w_stage.tile([P, N_TILE, PACK], BF16, align_bytes=64)
-                copy(
-                    out=grouped_w[:].rearrange("p (c i) t -> p c t i", i=4),
-                    in_=raw[:, g, :, half_cols(half)].rearrange("p t (c i) -> p c t i", i=4),
-                )
-                grouped_weights[(name, g, half)] = grouped_w
+        def regroup_weights(copy, w, g, half):
+            grouped_w = w_stage.tile([P, N_TILE, PACK], BF16, align_bytes=64)
+            copy(
+                out=grouped_w[:].rearrange("p (c i) t -> p c t i", i=4),
+                in_=w["raw"][:, g, :, half_cols(half)].rearrange("p t (c i) -> p c t i", i=4),
+            )
+            grouped_weights[(w["name"], g, half)] = grouped_w
 
-        def quantise_weights(name, codes, scales, g):
-            for half in range(N_HALVES):
-                nc.vector.quantize_mx(
-                    out=codes[:, g, half_cols(half)].bitcast(FP8X4),
-                    scales=scales[:, g, half_cols(half)],
-                    in_=grouped_weights[(name, g, half)][:].rearrange("p n t -> p (n t)"),
-                )
+        def quantise_weights(w, g, half):
+            nc.vector.quantize_mx(
+                out=w["codes"][:, g, half_cols(half)].bitcast(FP8X4),
+                scales=w["scales"][:, g, half_cols(half)],
+                in_=grouped_weights[(w["name"], g, half)][:].rearrange("p n t -> p (n t)"),
+            )
 
         grouped_tokens = {}
 
-        def transpose_tokens(grp):
-            words = x_raw[:, grp, :].bitcast(F32)
-            flipped = psum.tile([P, PACK, P], F32, tag="flip")
-            for c in range(PACK):
-                nc.tensor.transpose(flipped[:, c, :], words[:, c * P : (c + 1) * P], ident[:])
-            grouped_x = x_stage.tile([P, PASSES, P, PACK], BF16, align_bytes=64)
-            nc.scalar.copy(
-                out=grouped_x[:].bitcast(F32), in_=flipped[:].rearrange("p (g u) n -> p g n u", u=2)
-            )
-            grouped_tokens[grp] = grouped_x
+        def transpose_tokens(chunk):
+            grouped_x = x_stage.tile([P, SCENES, PASSES, P, PACK], BF16, align_bytes=64)
+            for b in range(SCENES):
+                words = x_raw[:, chunk, b, :].bitcast(F32)
+                flipped = psum.tile([P, PACK, P], F32, tag="bank")
+                for c in range(PACK):
+                    nc.tensor.transpose(flipped[:, c, :], words[:, tokens(c)], ident[:])
+                nc.scalar.copy(
+                    out=grouped_x[:, b].bitcast(F32), in_=flipped[:].rearrange("p (g u) n -> p g n u", u=2)
+                )
+            grouped_tokens[chunk] = grouped_x
 
-        def quantise_tokens(grp):
+        def quantise_tokens(chunk):
             nc.vector.quantize_mx(
-                out=x_codes[:, grp, :].bitcast(FP8X4),
-                scales=x_scales[:, grp, :],
-                in_=grouped_tokens[grp][:].rearrange("p g n t -> p (g n t)"),
+                out=x_codes[:, chunk, :].bitcast(FP8X4),
+                scales=x_scales[:, chunk, :],
+                in_=grouped_tokens[chunk][:].rearrange("p b g n t -> p (b g n t)"),
             )
 
-        weights_t = keep.tile([P, CHUNKS, SCENES, HEADS, VIEWS], F32)
+        weights_t = keep.tile([P, CHUNKS, HALVES, PACK, SCENES, VIEWS], F32)
         piece_shape = [P, PIECE_POS, VIEWS]
         exponents = {}
         piece_weights = {}
@@ -198,17 +200,17 @@ def tile_crossviewattention_pa_kernel(tc, x, scores, Wv, bv, Wo, bo, out):
             piece_weights[piece] = weights
 
         def softmax_transpose(piece):
-            flipped = psum.tile([P, PACK, P], F32, tag="flip")
+            flipped = psum.tile([P, PACK, P], F32, tag="bank")
             for c in range(PIECE_CHUNKS):
                 nc.tensor.transpose(flipped[:, c, :], piece_weights[piece][:, c, :], ident[:])
             chunks = slice(piece * PIECE_CHUNKS, (piece + 1) * PIECE_CHUNKS)
             nc.scalar.copy(
-                out=weights_t[:, chunks].rearrange("p c b h i -> p (c b) h i"),
-                in_=flipped[:, 0:PIECE_CHUNKS, :].rearrange("p c (b i h) -> p (c b) h i", b=SCENES, i=VIEWS),
+                out=weights_t[:, chunks].rearrange("p c f t b i -> p c (f t b i)"),
+                in_=flipped[:, 0:PIECE_CHUNKS, :],
             )
 
-        def piece_that_starts_at(grp):
-            piece, offset = divmod(grp, PIECE_GROUPS)
+        def piece_that_starts_at(unit):
+            piece, offset = divmod(unit, PIECE_CHUNKS)
             return piece if offset == 0 and 0 <= piece < PIECES else None
 
         bv_cols = keep.tile([P, HEADS], F32)
@@ -216,7 +218,7 @@ def tile_crossviewattention_pa_kernel(tc, x, scores, Wv, bv, Wo, bo, out):
         def bias_columns():
             bv_wide = keep.tile([P, P], F32)
             nc.vector.tensor_copy(out=bv_wide[:], in_=bv_rows[:])
-            flipped = psum.tile([P, PACK, P], F32, tag="flip")
+            flipped = psum.tile([P, PACK, P], F32, tag="bank")
             nc.tensor.transpose(flipped[:, 0, :], bv_wide[:], ident[:])
             nc.vector.tensor_copy(out=bv_cols[:], in_=flipped[:, 0, 0:HEADS])
 
@@ -224,141 +226,151 @@ def tile_crossviewattention_pa_kernel(tc, x, scores, Wv, bv, Wo, bo, out):
         mix_weights = {}
         mix_sums = {}
         mixed_tokens = {}
-        mixed_codes = {}
         out_sums = {}
 
-        def first_projection(grp):
-            v_rows = v_pool.tile([P, FEATURES], F32)
-            for half in range(N_HALVES):
-                acc = psum.tile([P, N_TILE], F32, tag="acc_v")
+        def half_and_chunk(unit):
+            return divmod(unit, CHUNKS)
+
+        def first_projection(unit):
+            half, chunk = half_and_chunk(unit)
+            v_rows = v_pool.tile([P, SCENES, N_TILE], F32)
+            for b in range(SCENES):
+                acc = psum.tile([P, N_TILE], F32, tag="bank")
                 for g in range(PASSES):
-                    toks = slice(g * P, (g + 1) * P)
                     nc.tensor.matmul_mx(
                         out=acc[:],
-                        lhsT=x_codes[:, grp, toks].bitcast(FP8X4),
-                        lhsT_scale=x_scales[:, grp, toks],
+                        lhsT=x_codes[:, chunk, tokens(b * PASSES + g)].bitcast(FP8X4),
+                        lhsT_scale=x_scales[:, chunk, tokens(b * PASSES + g)],
                         rhs=wv_codes[:, g, half_cols(half)].bitcast(FP8X4),
                         rhs_scale=wv_scales[:, g, half_cols(half)],
                         start=(g == 0),
                         stop=(g == PASSES - 1),
                     )
-                nc.scalar.copy(out=v_rows[:, half_cols(half)], in_=acc[:])
-            values[grp] = v_rows
+                nc.scalar.copy(out=v_rows[:, b, :], in_=acc[:])
+            values[unit] = v_rows
 
-        def build_mix_weights(grp):
-            c, b = chunk_and_scene(grp)
-            shape = [P, HEADS, GROUP_POS, VIEWS]
-            mixw = mixw_pool.tile(shape, F32)
-            nc.gpsimd.tensor_tensor(
-                out=mixw[:],
-                in0=weights_t[:, c, b, :, :].unsqueeze(2).to_broadcast(shape),
-                in1=block_mask[:].unsqueeze(1).to_broadcast(shape),
-                op=MULT,
-            )
-            mix_weights[grp] = mixw
+        def build_mix_weights(unit):
+            half, chunk = half_and_chunk(unit)
+            shape = [P, PACK, GROUP_POS, VIEWS]
+            mixw = mixw_pool.tile([P, SCENES, PACK, GROUP_POS, VIEWS], F32)
+            for b in range(SCENES):
+                nc.gpsimd.tensor_tensor(
+                    out=mixw[:, b],
+                    in0=weights_t[:, chunk, half, :, b, :].unsqueeze(2).to_broadcast(shape),
+                    in1=block_mask[:].unsqueeze(1).to_broadcast(shape),
+                    op=MULT,
+                )
+            mix_weights[unit] = mixw
 
-        def mix(grp):
+        def mix(unit):
             sums = []
-            for g in range(PASSES):
-                acc = psum.tile([P, PACK, P], F32, tag="acc_mix")
+            for b in range(SCENES):
+                acc = psum.tile([P, PACK, P], F32, tag="bank")
                 for t in range(PACK):
-                    h = g * PACK + t
                     nc.tensor.matmul(
                         out=acc[:, t, :],
-                        lhsT=values[grp][:, h * P : (h + 1) * P],
-                        rhs=mix_weights[grp][:, h, :, :].rearrange("p s i -> p (s i)"),
+                        lhsT=values[unit][:, b, tokens(t)],
+                        rhs=mix_weights[unit][:, b, t, :, :].rearrange("p s i -> p (s i)"),
                         start=True,
                         stop=True,
                     )
                 sums.append(acc)
-            mix_sums[grp] = sums
+            mix_sums[unit] = sums
 
-        def round_mixed(grp):
-            mixed = m_pool.tile([P, PASSES, P, PACK], BF16, align_bytes=64)
-            for g in range(PASSES):
+        def round_mixed(unit):
+            half, chunk = half_and_chunk(unit)
+            mixed = m_pool.tile([P, SCENES, P, PACK], BF16, align_bytes=64)
+            for b in range(SCENES):
                 nc.vector.tensor_tensor(
-                    out=mixed[:, g, :, :],
-                    in0=mix_sums[grp][g][:].rearrange("p t n -> p n t"),
-                    in1=bv_cols[:, g * PACK : (g + 1) * PACK].unsqueeze(1).to_broadcast([P, P, PACK]),
+                    out=mixed[:, b, :, :],
+                    in0=mix_sums[unit][b][:].rearrange("p t n -> p n t"),
+                    in1=bv_cols[:, half * PACK : (half + 1) * PACK].unsqueeze(1).to_broadcast([P, P, PACK]),
                     op=ADD,
                 )
-            mixed_tokens[grp] = mixed
+            mixed_tokens[unit] = mixed
 
-        def quantise_mixed(grp):
-            m_codes = m_pool.tile([P, PASSES * P], U32, align_bytes=64)
-            m_scales = m_pool.tile([P, PASSES * P], U8, align_bytes=64)
+        def quantise_mixed(unit):
+            half, chunk = half_and_chunk(unit)
             nc.vector.quantize_mx(
-                out=m_codes[:].bitcast(FP8X4),
-                scales=m_scales[:],
-                in_=mixed_tokens[grp][:].rearrange("p g n t -> p (g n t)"),
+                out=m_codes[:, half, chunk, :].bitcast(FP8X4),
+                scales=m_scales[:, half, chunk, :],
+                in_=mixed_tokens[unit][:].rearrange("p b n t -> p (b n t)"),
             )
-            mixed_codes[grp] = (m_codes, m_scales)
 
-        def second_projection(grp):
-            m_codes, m_scales = mixed_codes[grp]
-            sums = []
-            for half in range(N_HALVES):
-                acc = psum.tile([P, N_TILE], F32, tag="acc_y")
-                for g in range(PASSES):
-                    toks = slice(g * P, (g + 1) * P)
-                    nc.tensor.matmul_mx(
-                        out=acc[:],
-                        lhsT=m_codes[:, toks].bitcast(FP8X4),
-                        lhsT_scale=m_scales[:, toks],
-                        rhs=wo_codes[:, g, half_cols(half)].bitcast(FP8X4),
-                        rhs_scale=wo_scales[:, g, half_cols(half)],
-                        start=(g == 0),
-                        stop=(g == PASSES - 1),
+        def second_projection(chunk):
+            sums = {}
+            for b in range(SCENES):
+                for half in range(HALVES):
+                    acc = psum.tile([P, N_TILE], F32, tag="bank")
+                    for g in range(PASSES):
+                        nc.tensor.matmul_mx(
+                            out=acc[:],
+                            lhsT=m_codes[:, g, chunk, tokens(b)].bitcast(FP8X4),
+                            lhsT_scale=m_scales[:, g, chunk, tokens(b)],
+                            rhs=wo_codes[:, g, half_cols(half)].bitcast(FP8X4),
+                            rhs_scale=wo_scales[:, g, half_cols(half)],
+                            start=(g == 0),
+                            stop=(g == PASSES - 1),
+                        )
+                    sums[(b, half)] = acc
+            out_sums[chunk] = sums
+
+        def finish(chunk):
+            for b in range(SCENES):
+                for half in range(HALVES):
+                    result = y_pool.tile([P, N_TILE], F32)
+                    nc.vector.tensor_tensor(
+                        out=result[:], in0=out_sums[chunk][(b, half)][:], in1=bo_all[:, half_cols(half)], op=ADD
                     )
-                sums.append(acc)
-            out_sums[grp] = sums
+                    nc.sync.dma_start(out=group_rows(out, chunk, b, half_cols(half)), in_=result[:])
 
-        def finish(grp):
-            for half in range(N_HALVES):
-                result = y_pool.tile([P, N_TILE], F32)
-                nc.vector.tensor_tensor(
-                    out=result[:], in0=out_sums[grp][half][:], in1=bo_all[:, half_cols(half)], op=ADD
-                )
-                nc.sync.dma_start(out=group_rows(out, grp, half_cols(half)), in_=result[:])
+        def is_unit(unit):
+            return 0 <= unit < UNITS
 
-        def is_group(grp):
-            return 0 <= grp < GROUPS
+        def is_chunk(chunk):
+            return 0 <= chunk < CHUNKS
 
         def is_pass(g):
             return 0 <= g < PASSES
 
         wv_start = -(AHEAD_V + AHEAD_X)
-        wo_start = BEHIND_Y - PASSES - 1
-        for step in range(FIRST_STEP, GROUPS + BEHIND_Y):
-            if is_group(step - 1):
+        later_halves = [(wv_tiles, 1), (wo_tiles, 0), (wo_tiles, 1)]
+        later_start = 3
+        for step in range(FIRST_STEP, LAST_STEP + 1):
+            later, second_step = divmod(step - later_start, 2)
+            is_later = 0 <= later < len(later_halves)
+
+            if is_unit(step - 1):
                 round_mixed(step - 1)
-            if is_group(step - BEHIND_Y):
-                second_projection(step - BEHIND_Y)
-                finish(step - BEHIND_Y)
-            if is_group(step - 1):
+            if is_chunk(step - UNITS - BEHIND_Y + CHUNKS):
+                second_projection(step - UNITS - BEHIND_Y + CHUNKS)
+                finish(step - UNITS - BEHIND_Y + CHUNKS)
+            if is_unit(step - 1):
                 quantise_mixed(step - 1)
             if is_pass(step - wv_start - 1):
-                quantise_weights("wv", wv_codes, wv_scales, step - wv_start - 1)
-            if is_pass(step - wo_start - 1):
-                quantise_weights("wo", wo_codes, wo_scales, step - wo_start - 1)
-            if is_group(step + AHEAD_V):
+                quantise_weights(wv_tiles, step - wv_start - 1, 0)
+            if is_later and second_step == 1:
+                for g in range(PASSES):
+                    quantise_weights(later_halves[later][0], g, later_halves[later][1])
+            if is_chunk(step + AHEAD_V + AHEAD_X - 1):
+                quantise_tokens(step + AHEAD_V + AHEAD_X - 1)
+            if is_unit(step + AHEAD_V):
                 first_projection(step + AHEAD_V)
 
             piece = piece_that_starts_at(step + AHEAD_W + 2)
             if piece is not None:
                 softmax_exp(piece)
             if is_pass(step - wv_start):
-                regroup_weights("wv", wv_raw, step - wv_start)
-            if is_pass(step - wo_start):
-                regroup_weights("wo", wo_raw, step - wo_start)
+                regroup_weights(nc.vector.tensor_copy, wv_tiles, step - wv_start, 0)
+            if is_later and second_step == 0:
+                regroup_weights(nc.scalar.copy, later_halves[later][0], 0, later_halves[later][1])
+                regroup_weights(nc.vector.tensor_copy, later_halves[later][0], 1, later_halves[later][1])
 
-            if is_group(step + AHEAD_V + AHEAD_X):
-                transpose_tokens(step + AHEAD_V + AHEAD_X)
             piece = piece_that_starts_at(step + AHEAD_W + 1)
             if piece is not None:
                 softmax_transpose(piece)
-            if is_group(step + AHEAD_V + AHEAD_X - 1):
-                quantise_tokens(step + AHEAD_V + AHEAD_X - 1)
+            if is_chunk(step + AHEAD_V + AHEAD_X):
+                transpose_tokens(step + AHEAD_V + AHEAD_X)
             if step == -AHEAD_V:
                 bias_columns()
 
@@ -369,7 +381,7 @@ def tile_crossviewattention_pa_kernel(tc, x, scores, Wv, bv, Wo, bo, out):
             if piece is not None:
                 softmax_shift(piece)
 
-            if is_group(step + AHEAD_W):
+            if is_unit(step + AHEAD_W):
                 build_mix_weights(step + AHEAD_W)
-            if is_group(step):
+            if is_unit(step):
                 mix(step)

@@ -21,21 +21,21 @@ PACK = 4
 K_PASS = P * PACK
 PASSES = FEATURES // K_PASS
 N_TILE = 512
-HALVES = FEATURES // N_TILE
+N_HALVES = FEATURES // N_TILE
 GROUP_POS = P // VIEWS
 CHUNKS = POSITIONS // GROUP_POS
-UNITS = HALVES * CHUNKS
+GROUPS = SCENES * CHUNKS
 
 PIECE_CHUNKS = 2
+PIECE_GROUPS = PIECE_CHUNKS * SCENES
 PIECE_POS = PIECE_CHUNKS * GROUP_POS
 PIECES = CHUNKS // PIECE_CHUNKS
 
-AHEAD_V = 1
+AHEAD_V = 2
 AHEAD_X = 2
-AHEAD_W = 1
-BEHIND_Y = 2
+AHEAD_W = 2
+BEHIND_Y = 3
 FIRST_STEP = -(AHEAD_W + 3)
-LAST_STEP = UNITS + BEHIND_Y - 1
 
 FLOPS = 2 * 2 * SCENES * VIEWS * POSITIONS * FEATURES * FEATURES + 2 * SCENES * VIEWS * VIEWS * POSITIONS * FEATURES
 
@@ -49,40 +49,37 @@ def tile_crossviewattention_pa_kernel(tc, x, scores, Wv, bv, Wo, bo, out):
         s_pool = ctx.enter_context(tc.tile_pool(name="s_pool", bufs=2))
         v_pool = ctx.enter_context(tc.tile_pool(name="v_pool", bufs=AHEAD_V + 2))
         mixw_pool = ctx.enter_context(tc.tile_pool(name="mixw_pool", bufs=AHEAD_W + 2))
-        m_pool = ctx.enter_context(tc.tile_pool(name="m_pool", bufs=3))
-        y_pool = ctx.enter_context(tc.tile_pool(name="y_pool", bufs=8))
-        psum = ctx.enter_context(tc.psum_pool(name="psum", bufs=8))
+        m_pool = ctx.enter_context(tc.tile_pool(name="m_pool", bufs=BEHIND_Y + 2))
+        y_pool = ctx.enter_context(tc.tile_pool(name="y_pool", bufs=6))
+        psum = ctx.enter_context(tc.psum_pool(name="psum", bufs=2))
         ctx.enter_context(tc.manual_schedule())
 
-        def group_rows(dram, chunk, b, cols):
-            block = dram[b * VIEWS : (b + 1) * VIEWS, chunk * GROUP_POS : (chunk + 1) * GROUP_POS, cols]
+        def chunk_and_scene(grp):
+            return divmod(grp, SCENES)
+
+        def group_rows(dram, grp, cols):
+            c, b = chunk_and_scene(grp)
+            block = dram[b * VIEWS : (b + 1) * VIEWS, c * GROUP_POS : (c + 1) * GROUP_POS, cols]
             return block.rearrange("j s k -> s j k")
 
         def half_cols(half):
             return slice(half * N_TILE, (half + 1) * N_TILE)
 
-        def tokens(index):
-            return slice(index * P, (index + 1) * P)
-
-        x_raw = keep.tile([P, CHUNKS, SCENES, FEATURES], BF16)
-        x_codes = keep.tile([P, CHUNKS, SCENES * PASSES * P], U32, align_bytes=64)
-        x_scales = keep.tile([P, CHUNKS, SCENES * PASSES * P], U8, align_bytes=64)
-        m_codes = keep.tile([P, PASSES, CHUNKS, SCENES * P], U32, align_bytes=64)
-        m_scales = keep.tile([P, PASSES, CHUNKS, SCENES * P], U8, align_bytes=64)
+        x_raw = keep.tile([P, GROUPS, FEATURES], BF16)
+        x_codes = keep.tile([P, GROUPS, PASSES * P], U32, align_bytes=64)
+        x_scales = keep.tile([P, GROUPS, PASSES * P], U8, align_bytes=64)
         wv_raw = keep.tile([P, PASSES, PACK, FEATURES], BF16)
         wv_codes = keep.tile([P, PASSES, FEATURES], U32, align_bytes=64)
         wv_scales = keep.tile([P, PASSES, FEATURES], U8, align_bytes=64)
         wo_raw = keep.tile([P, PASSES, PACK, FEATURES], BF16)
         wo_codes = keep.tile([P, PASSES, FEATURES], U32, align_bytes=64)
         wo_scales = keep.tile([P, PASSES, FEATURES], U8, align_bytes=64)
-        wv_tiles = {"name": "wv", "raw": wv_raw, "codes": wv_codes, "scales": wv_scales}
-        wo_tiles = {"name": "wo", "raw": wo_raw, "codes": wo_codes, "scales": wo_scales}
         score_raw = keep.tile([P, VIEWS, POSITIONS], BF16)
         bv_rows = keep.tile([P, P], BF16)
         bo_all = keep.tile([P, FEATURES], BF16)
 
-        def load_tokens(chunk, b):
-            nc.sync.dma_start(out=x_raw[:, chunk, b, :], in_=group_rows(x, chunk, b, slice(0, FEATURES)))
+        def load_tokens(grp):
+            nc.sync.dma_start(out=x_raw[:, grp, :], in_=group_rows(x, grp, slice(0, FEATURES)))
 
         def load_wv(g):
             nc.sync.dma_start(
@@ -96,26 +93,28 @@ def tile_crossviewattention_pa_kernel(tc, x, scores, Wv, bv, Wo, bo, out):
                 in_=Wo[g * K_PASS : (g + 1) * K_PASS, :].rearrange("(t p) n -> p t n", p=P),
             )
 
-        def load_scores(j):
-            nc.scalar.dma_start(
-                out=score_raw[:, j, :], in_=scores[:, :, j, :, :].rearrange("b i h s -> h (b i) s")
+        def load_scores(queue, j):
+            queue.dma_start(
+                out=score_raw[:, j, :], in_=scores[:, :, j, :, :].rearrange("b i h s -> (b i) h s")
             )
 
         nc.vector.memset(bv_rows[:], 0.0)
-        for j in range(VIEWS - 2):
-            load_scores(j)
-        load_tokens(0, 0)
+        for j in range(VIEWS):
+            load_scores(nc.scalar if j < VIEWS - 2 else nc.gpsimd, j)
+        warm = keep.tile([P, 1], F32)
+        nc.vector.memset(warm[:], 0.0)
+        nc.scalar.activation(out=warm[:], in_=warm[:], func=EXP)
+        load_tokens(0)
         load_wv(0)
-        for j in range(VIEWS - 2, VIEWS):
-            load_scores(j)
-        load_tokens(0, 1)
+        load_tokens(1)
         load_wv(1)
         nc.scalar.dma_start(out=bv_rows[0:HEADS, :], in_=bv.rearrange("(h c) -> h c", c=P))
-        for chunk in range(1, CHUNKS):
-            for b in range(SCENES):
-                load_tokens(chunk, b)
+        for grp in range(2, AHEAD_V + AHEAD_X):
+            load_tokens(grp)
         for g in range(PASSES):
             load_wo(g)
+        for grp in range(AHEAD_V + AHEAD_X, GROUPS):
+            load_tokens(grp)
         nc.sync.dma_start(out=bo_all[:], in_=bo.partition_broadcast(P))
 
         ident = keep.tile([P, P], F32)
@@ -131,43 +130,50 @@ def tile_crossviewattention_pa_kernel(tc, x, scores, Wv, bv, Wo, bo, out):
 
         grouped_weights = {}
 
-        def regroup_weights(copy, w, g, half):
-            grouped_w = w_stage.tile([P, N_TILE, PACK], BF16, align_bytes=64)
-            copy(
-                out=grouped_w[:].rearrange("p (c i) t -> p c t i", i=4),
-                in_=w["raw"][:, g, :, half_cols(half)].rearrange("p t (c i) -> p c t i", i=4),
-            )
-            grouped_weights[(w["name"], g, half)] = grouped_w
+        def regroup_weights(name, raw, g):
+            for half, copy in enumerate((nc.vector.tensor_copy, nc.scalar.copy)):
+                grouped_w = w_stage.tile([P, N_TILE, PACK], BF16, align_bytes=64)
+                copy(
+                    out=grouped_w[:].rearrange("p (c i) t -> p c t i", i=4),
+                    in_=raw[:, g, :, half_cols(half)].rearrange("p t (c i) -> p c t i", i=4),
+                )
+                grouped_weights[(name, g, half)] = grouped_w
 
-        def quantise_weights(w, g, half):
-            nc.vector.quantize_mx(
-                out=w["codes"][:, g, half_cols(half)].bitcast(FP8X4),
-                scales=w["scales"][:, g, half_cols(half)],
-                in_=grouped_weights[(w["name"], g, half)][:].rearrange("p n t -> p (n t)"),
-            )
+        def quantise_weights(name, codes, scales, g):
+            for half in range(N_HALVES):
+                nc.vector.quantize_mx(
+                    out=codes[:, g, half_cols(half)].bitcast(FP8X4),
+                    scales=scales[:, g, half_cols(half)],
+                    in_=grouped_weights[(name, g, half)][:].rearrange("p n t -> p (n t)"),
+                )
 
         grouped_tokens = {}
 
         def transpose_tokens(chunk):
             grouped_x = x_stage.tile([P, SCENES, PASSES, P, PACK], BF16, align_bytes=64)
             for b in range(SCENES):
-                words = x_raw[:, chunk, b, :].bitcast(F32)
-                flipped = psum.tile([P, PACK, P], F32, tag="bank")
+                words = x_raw[:, chunk * SCENES + b, :].bitcast(F32)
+                flipped = psum.tile([P, PACK, P], F32, tag="flip")
                 for c in range(PACK):
-                    nc.tensor.transpose(flipped[:, c, :], words[:, tokens(c)], ident[:])
+                    nc.tensor.transpose(flipped[:, c, :], words[:, c * P : (c + 1) * P], ident[:])
                 nc.scalar.copy(
                     out=grouped_x[:, b].bitcast(F32), in_=flipped[:].rearrange("p (g u) n -> p g n u", u=2)
                 )
             grouped_tokens[chunk] = grouped_x
 
         def quantise_tokens(chunk):
+            groups = slice(chunk * SCENES, (chunk + 1) * SCENES)
             nc.vector.quantize_mx(
-                out=x_codes[:, chunk, :].bitcast(FP8X4),
-                scales=x_scales[:, chunk, :],
+                out=x_codes[:, groups, :].rearrange("p b w -> p (b w)").bitcast(FP8X4),
+                scales=x_scales[:, groups, :].rearrange("p b w -> p (b w)"),
                 in_=grouped_tokens[chunk][:].rearrange("p b g n t -> p (b g n t)"),
             )
 
-        weights_t = keep.tile([P, CHUNKS, HALVES, PACK, SCENES, VIEWS], F32)
+        def chunk_that_starts_at(grp):
+            chunk, offset = divmod(grp, SCENES)
+            return chunk if offset == 0 and 0 <= chunk < CHUNKS else None
+
+        weights_t = keep.tile([P, CHUNKS, SCENES, HEADS, VIEWS], F32)
         piece_shape = [P, PIECE_POS, VIEWS]
         exponents = {}
         piece_weights = {}
@@ -200,17 +206,17 @@ def tile_crossviewattention_pa_kernel(tc, x, scores, Wv, bv, Wo, bo, out):
             piece_weights[piece] = weights
 
         def softmax_transpose(piece):
-            flipped = psum.tile([P, PACK, P], F32, tag="bank")
+            flipped = psum.tile([P, PACK, P], F32, tag="flip")
             for c in range(PIECE_CHUNKS):
                 nc.tensor.transpose(flipped[:, c, :], piece_weights[piece][:, c, :], ident[:])
             chunks = slice(piece * PIECE_CHUNKS, (piece + 1) * PIECE_CHUNKS)
             nc.scalar.copy(
-                out=weights_t[:, chunks].rearrange("p c f t b i -> p c (f t b i)"),
-                in_=flipped[:, 0:PIECE_CHUNKS, :],
+                out=weights_t[:, chunks].rearrange("p c b h i -> p (c b) h i"),
+                in_=flipped[:, 0:PIECE_CHUNKS, :].rearrange("p c (b i h) -> p (c b) h i", b=SCENES, i=VIEWS),
             )
 
-        def piece_that_starts_at(unit):
-            piece, offset = divmod(unit, PIECE_CHUNKS)
+        def piece_that_starts_at(grp):
+            piece, offset = divmod(grp, PIECE_GROUPS)
             return piece if offset == 0 and 0 <= piece < PIECES else None
 
         bv_cols = keep.tile([P, HEADS], F32)
@@ -218,7 +224,7 @@ def tile_crossviewattention_pa_kernel(tc, x, scores, Wv, bv, Wo, bo, out):
         def bias_columns():
             bv_wide = keep.tile([P, P], F32)
             nc.vector.tensor_copy(out=bv_wide[:], in_=bv_rows[:])
-            flipped = psum.tile([P, PACK, P], F32, tag="bank")
+            flipped = psum.tile([P, PACK, P], F32, tag="flip")
             nc.tensor.transpose(flipped[:, 0, :], bv_wide[:], ident[:])
             nc.vector.tensor_copy(out=bv_cols[:], in_=flipped[:, 0, 0:HEADS])
 
@@ -226,151 +232,145 @@ def tile_crossviewattention_pa_kernel(tc, x, scores, Wv, bv, Wo, bo, out):
         mix_weights = {}
         mix_sums = {}
         mixed_tokens = {}
+        mixed_codes = {}
         out_sums = {}
 
-        def half_and_chunk(unit):
-            return divmod(unit, CHUNKS)
-
-        def first_projection(unit):
-            half, chunk = half_and_chunk(unit)
-            v_rows = v_pool.tile([P, SCENES, N_TILE], F32)
-            for b in range(SCENES):
-                acc = psum.tile([P, N_TILE], F32, tag="bank")
+        def first_projection(grp):
+            v_rows = v_pool.tile([P, FEATURES], F32)
+            for half in range(N_HALVES):
+                acc = psum.tile([P, N_TILE], F32, tag="acc_v")
                 for g in range(PASSES):
+                    toks = slice(g * P, (g + 1) * P)
                     nc.tensor.matmul_mx(
                         out=acc[:],
-                        lhsT=x_codes[:, chunk, tokens(b * PASSES + g)].bitcast(FP8X4),
-                        lhsT_scale=x_scales[:, chunk, tokens(b * PASSES + g)],
+                        lhsT=x_codes[:, grp, toks].bitcast(FP8X4),
+                        lhsT_scale=x_scales[:, grp, toks],
                         rhs=wv_codes[:, g, half_cols(half)].bitcast(FP8X4),
                         rhs_scale=wv_scales[:, g, half_cols(half)],
                         start=(g == 0),
                         stop=(g == PASSES - 1),
                     )
-                nc.scalar.copy(out=v_rows[:, b, :], in_=acc[:])
-            values[unit] = v_rows
+                nc.scalar.copy(out=v_rows[:, half_cols(half)], in_=acc[:])
+            values[grp] = v_rows
 
-        def build_mix_weights(unit):
-            half, chunk = half_and_chunk(unit)
+        def build_mix_weights(grp):
+            c, b = chunk_and_scene(grp)
             shape = [P, PACK, GROUP_POS, VIEWS]
-            mixw = mixw_pool.tile([P, SCENES, PACK, GROUP_POS, VIEWS], F32)
-            for b in range(SCENES):
+            mixw = mixw_pool.tile([P, HEADS, GROUP_POS, VIEWS], F32)
+            for g in range(PASSES):
+                heads = slice(g * PACK, (g + 1) * PACK)
                 nc.gpsimd.tensor_tensor(
-                    out=mixw[:, b],
-                    in0=weights_t[:, chunk, half, :, b, :].unsqueeze(2).to_broadcast(shape),
+                    out=mixw[:, heads],
+                    in0=weights_t[:, c, b, heads, :].unsqueeze(2).to_broadcast(shape),
                     in1=block_mask[:].unsqueeze(1).to_broadcast(shape),
                     op=MULT,
                 )
-            mix_weights[unit] = mixw
+            mix_weights[grp] = mixw
 
-        def mix(unit):
+        def mix(grp):
             sums = []
-            for b in range(SCENES):
-                acc = psum.tile([P, PACK, P], F32, tag="bank")
+            for g in range(PASSES):
+                acc = psum.tile([P, PACK, P], F32, tag="acc_mix")
                 for t in range(PACK):
+                    h = g * PACK + t
                     nc.tensor.matmul(
                         out=acc[:, t, :],
-                        lhsT=values[unit][:, b, tokens(t)],
-                        rhs=mix_weights[unit][:, b, t, :, :].rearrange("p s i -> p (s i)"),
+                        lhsT=values[grp][:, h * P : (h + 1) * P],
+                        rhs=mix_weights[grp][:, h, :, :].rearrange("p s i -> p (s i)"),
                         start=True,
                         stop=True,
                     )
                 sums.append(acc)
-            mix_sums[unit] = sums
+            mix_sums[grp] = sums
 
-        def round_mixed(unit):
-            half, chunk = half_and_chunk(unit)
-            mixed = m_pool.tile([P, SCENES, P, PACK], BF16, align_bytes=64)
-            for b in range(SCENES):
+        def round_mixed(grp):
+            mixed = m_pool.tile([P, PASSES, P, PACK], BF16, align_bytes=64)
+            for g in range(PASSES):
                 nc.vector.tensor_tensor(
-                    out=mixed[:, b, :, :],
-                    in0=mix_sums[unit][b][:].rearrange("p t n -> p n t"),
-                    in1=bv_cols[:, half * PACK : (half + 1) * PACK].unsqueeze(1).to_broadcast([P, P, PACK]),
+                    out=mixed[:, g, :, :],
+                    in0=mix_sums[grp][g][:].rearrange("p t n -> p n t"),
+                    in1=bv_cols[:, g * PACK : (g + 1) * PACK].unsqueeze(1).to_broadcast([P, P, PACK]),
                     op=ADD,
                 )
-            mixed_tokens[unit] = mixed
+            mixed_tokens[grp] = mixed
 
-        def quantise_mixed(unit):
-            half, chunk = half_and_chunk(unit)
+        def quantise_mixed(grp):
+            m_codes = m_pool.tile([P, PASSES * P], U32, align_bytes=64)
+            m_scales = m_pool.tile([P, PASSES * P], U8, align_bytes=64)
             nc.vector.quantize_mx(
-                out=m_codes[:, half, chunk, :].bitcast(FP8X4),
-                scales=m_scales[:, half, chunk, :],
-                in_=mixed_tokens[unit][:].rearrange("p b n t -> p (b n t)"),
+                out=m_codes[:].bitcast(FP8X4),
+                scales=m_scales[:],
+                in_=mixed_tokens[grp][:].rearrange("p g n t -> p (g n t)"),
             )
+            mixed_codes[grp] = (m_codes, m_scales)
 
-        def second_projection(chunk):
-            sums = {}
-            for b in range(SCENES):
-                for half in range(HALVES):
-                    acc = psum.tile([P, N_TILE], F32, tag="bank")
-                    for g in range(PASSES):
-                        nc.tensor.matmul_mx(
-                            out=acc[:],
-                            lhsT=m_codes[:, g, chunk, tokens(b)].bitcast(FP8X4),
-                            lhsT_scale=m_scales[:, g, chunk, tokens(b)],
-                            rhs=wo_codes[:, g, half_cols(half)].bitcast(FP8X4),
-                            rhs_scale=wo_scales[:, g, half_cols(half)],
-                            start=(g == 0),
-                            stop=(g == PASSES - 1),
-                        )
-                    sums[(b, half)] = acc
-            out_sums[chunk] = sums
-
-        def finish(chunk):
-            for b in range(SCENES):
-                for half in range(HALVES):
-                    result = y_pool.tile([P, N_TILE], F32)
-                    nc.vector.tensor_tensor(
-                        out=result[:], in0=out_sums[chunk][(b, half)][:], in1=bo_all[:, half_cols(half)], op=ADD
+        def second_projection(grp):
+            m_codes, m_scales = mixed_codes[grp]
+            sums = []
+            for half in range(N_HALVES):
+                acc = psum.tile([P, N_TILE], F32, tag="acc_y")
+                for g in range(PASSES):
+                    toks = slice(g * P, (g + 1) * P)
+                    nc.tensor.matmul_mx(
+                        out=acc[:],
+                        lhsT=m_codes[:, toks].bitcast(FP8X4),
+                        lhsT_scale=m_scales[:, toks],
+                        rhs=wo_codes[:, g, half_cols(half)].bitcast(FP8X4),
+                        rhs_scale=wo_scales[:, g, half_cols(half)],
+                        start=(g == 0),
+                        stop=(g == PASSES - 1),
                     )
-                    nc.sync.dma_start(out=group_rows(out, chunk, b, half_cols(half)), in_=result[:])
+                sums.append(acc)
+            out_sums[grp] = sums
 
-        def is_unit(unit):
-            return 0 <= unit < UNITS
+        def finish(grp):
+            for half in range(N_HALVES):
+                result = y_pool.tile([P, N_TILE], F32)
+                nc.vector.tensor_tensor(
+                    out=result[:], in0=out_sums[grp][half][:], in1=bo_all[:, half_cols(half)], op=ADD
+                )
+                nc.sync.dma_start(out=group_rows(out, grp, half_cols(half)), in_=result[:])
 
-        def is_chunk(chunk):
-            return 0 <= chunk < CHUNKS
+        def is_group(grp):
+            return 0 <= grp < GROUPS
 
         def is_pass(g):
             return 0 <= g < PASSES
 
         wv_start = -(AHEAD_V + AHEAD_X)
-        later_halves = [(wv_tiles, 1), (wo_tiles, 0), (wo_tiles, 1)]
-        later_start = 3
-        for step in range(FIRST_STEP, LAST_STEP + 1):
-            later, second_step = divmod(step - later_start, 2)
-            is_later = 0 <= later < len(later_halves)
-
-            if is_unit(step - 1):
+        wo_start = BEHIND_Y - PASSES - 1
+        for step in range(FIRST_STEP, GROUPS + BEHIND_Y):
+            if is_group(step - 1):
                 round_mixed(step - 1)
-            if is_chunk(step - UNITS - BEHIND_Y + CHUNKS):
-                second_projection(step - UNITS - BEHIND_Y + CHUNKS)
-                finish(step - UNITS - BEHIND_Y + CHUNKS)
-            if is_unit(step - 1):
+            if is_group(step - BEHIND_Y):
+                second_projection(step - BEHIND_Y)
+                finish(step - BEHIND_Y)
+            if is_group(step - 1):
                 quantise_mixed(step - 1)
             if is_pass(step - wv_start - 1):
-                quantise_weights(wv_tiles, step - wv_start - 1, 0)
-            if is_later and second_step == 1:
-                for g in range(PASSES):
-                    quantise_weights(later_halves[later][0], g, later_halves[later][1])
-            if is_chunk(step + AHEAD_V + AHEAD_X - 1):
-                quantise_tokens(step + AHEAD_V + AHEAD_X - 1)
-            if is_unit(step + AHEAD_V):
+                quantise_weights("wv", wv_codes, wv_scales, step - wv_start - 1)
+            if is_pass(step - wo_start - 1):
+                quantise_weights("wo", wo_codes, wo_scales, step - wo_start - 1)
+            if is_group(step + AHEAD_V):
                 first_projection(step + AHEAD_V)
 
             piece = piece_that_starts_at(step + AHEAD_W + 2)
             if piece is not None:
                 softmax_exp(piece)
             if is_pass(step - wv_start):
-                regroup_weights(nc.vector.tensor_copy, wv_tiles, step - wv_start, 0)
-            if is_later and second_step == 0:
-                regroup_weights(nc.scalar.copy, later_halves[later][0], 0, later_halves[later][1])
-                regroup_weights(nc.vector.tensor_copy, later_halves[later][0], 1, later_halves[later][1])
+                regroup_weights("wv", wv_raw, step - wv_start)
+            if is_pass(step - wo_start):
+                regroup_weights("wo", wo_raw, step - wo_start)
 
             piece = piece_that_starts_at(step + AHEAD_W + 1)
             if piece is not None:
                 softmax_transpose(piece)
-            if is_chunk(step + AHEAD_V + AHEAD_X):
-                transpose_tokens(step + AHEAD_V + AHEAD_X)
+            chunk = chunk_that_starts_at(step + AHEAD_V + AHEAD_X)
+            if chunk is not None:
+                transpose_tokens(chunk)
+            chunk = chunk_that_starts_at(step + AHEAD_V + AHEAD_X - 1)
+            if chunk is not None:
+                quantise_tokens(chunk)
             if step == -AHEAD_V:
                 bias_columns()
 
@@ -381,7 +381,7 @@ def tile_crossviewattention_pa_kernel(tc, x, scores, Wv, bv, Wo, bo, out):
             if piece is not None:
                 softmax_shift(piece)
 
-            if is_unit(step + AHEAD_W):
+            if is_group(step + AHEAD_W):
                 build_mix_weights(step + AHEAD_W)
-            if is_unit(step):
+            if is_group(step):
                 mix(step)

from contextlib import ExitStack

import concourse.mybir as mybir
from concourse.masks import make_identity

F32 = mybir.dt.float32
BF16 = mybir.dt.bfloat16
U32 = mybir.dt.uint32
U8 = mybir.dt.uint8
FP8X4 = mybir.dt.float8_e4m3fn_x4
ADD = mybir.AluOpType.add
SUBTRACT = mybir.AluOpType.subtract
MULT = mybir.AluOpType.mult
MAX = mybir.AluOpType.max
INNERMOST = mybir.AxisListType.X
EXP = mybir.ActivationFunctionType.Exp

P = 128
SCENES, VIEWS, POSITIONS, FEATURES, HEADS = 2, 8, 128, 1024, 8
PACK = 4
K_PASS = P * PACK
PASSES = FEATURES // K_PASS
N_TILE = 512
N_HALVES = FEATURES // N_TILE
GROUP_POS = P // VIEWS
CHUNKS = POSITIONS // GROUP_POS
GROUPS = SCENES * CHUNKS

PIECE_CHUNKS = 2
PIECE_GROUPS = PIECE_CHUNKS * SCENES
PIECE_POS = PIECE_CHUNKS * GROUP_POS
PIECES = CHUNKS // PIECE_CHUNKS

AHEAD_V = 2
AHEAD_X = 2
AHEAD_W = 2
BEHIND_Y = 3
FIRST_STEP = -(AHEAD_W + 3)

FLOPS = 2 * 2 * SCENES * VIEWS * POSITIONS * FEATURES * FEATURES + 2 * SCENES * VIEWS * VIEWS * POSITIONS * FEATURES


def tile_crossviewattention_pa_kernel(tc, x, scores, Wv, bv, Wo, bo, out):
    nc = tc.nc
    with ExitStack() as ctx:
        keep = ctx.enter_context(tc.tile_pool(name="keep", bufs=1))
        x_stage = ctx.enter_context(tc.tile_pool(name="x_stage", bufs=3))
        w_stage = ctx.enter_context(tc.tile_pool(name="w_stage", bufs=4))
        s_pool = ctx.enter_context(tc.tile_pool(name="s_pool", bufs=2))
        v_pool = ctx.enter_context(tc.tile_pool(name="v_pool", bufs=AHEAD_V + 2))
        mixw_pool = ctx.enter_context(tc.tile_pool(name="mixw_pool", bufs=AHEAD_W + 2))
        m_pool = ctx.enter_context(tc.tile_pool(name="m_pool", bufs=BEHIND_Y + 2))
        y_pool = ctx.enter_context(tc.tile_pool(name="y_pool", bufs=6))
        psum = ctx.enter_context(tc.psum_pool(name="psum", bufs=2))
        ctx.enter_context(tc.manual_schedule())

        def chunk_and_scene(grp):
            return divmod(grp, SCENES)

        def group_rows(dram, grp, cols):
            c, b = chunk_and_scene(grp)
            block = dram[b * VIEWS : (b + 1) * VIEWS, c * GROUP_POS : (c + 1) * GROUP_POS, cols]
            return block.rearrange("j s k -> s j k")

        def half_cols(half):
            return slice(half * N_TILE, (half + 1) * N_TILE)

        x_raw = keep.tile([P, GROUPS, FEATURES], BF16)
        x_codes = keep.tile([P, GROUPS, PASSES * P], U32, align_bytes=64)
        x_scales = keep.tile([P, GROUPS, PASSES * P], U8, align_bytes=64)
        wv_raw = keep.tile([P, PASSES, PACK, FEATURES], BF16)
        wv_codes = keep.tile([P, PASSES, FEATURES], U32, align_bytes=64)
        wv_scales = keep.tile([P, PASSES, FEATURES], U8, align_bytes=64)
        wo_raw = keep.tile([P, PASSES, PACK, FEATURES], BF16)
        wo_codes = keep.tile([P, PASSES, FEATURES], U32, align_bytes=64)
        wo_scales = keep.tile([P, PASSES, FEATURES], U8, align_bytes=64)
        score_raw = keep.tile([P, VIEWS, POSITIONS], BF16)
        bv_rows = keep.tile([P, P], BF16)
        bo_all = keep.tile([P, FEATURES], BF16)

        def load_tokens(grp):
            nc.sync.dma_start(out=x_raw[:, grp, :], in_=group_rows(x, grp, slice(0, FEATURES)))

        def load_wv(g):
            nc.sync.dma_start(
                out=wv_raw[:, g, :, :].rearrange("p (u e) n -> p u (e n)", e=2),
                in_=Wv[g * K_PASS : (g + 1) * K_PASS, :].rearrange("(u p e) n -> p u (e n)", u=2, e=2),
            )

        def load_wo(g):
            nc.sync.dma_start(
                out=wo_raw[:, g, :, :],
                in_=Wo[g * K_PASS : (g + 1) * K_PASS, :].rearrange("(t p) n -> p t n", p=P),
            )

        def load_scores(queue, j):
            queue.dma_start(
                out=score_raw[:, j, :], in_=scores[:, :, j, :, :].rearrange("b i h s -> (b i) h s")
            )

        nc.vector.memset(bv_rows[:], 0.0)
        for j in range(VIEWS):
            load_scores(nc.scalar if j < VIEWS - 2 else nc.gpsimd, j)
        warm = keep.tile([P, 1], F32)
        nc.vector.memset(warm[:], 0.0)
        nc.scalar.activation(out=warm[:], in_=warm[:], func=EXP)
        load_tokens(0)
        load_wv(0)
        load_tokens(1)
        load_wv(1)
        nc.scalar.dma_start(out=bv_rows[0:HEADS, :], in_=bv.rearrange("(h c) -> h c", c=P))
        for grp in range(2, AHEAD_V + AHEAD_X):
            load_tokens(grp)
        for g in range(PASSES):
            load_wo(g)
        for grp in range(AHEAD_V + AHEAD_X, GROUPS):
            load_tokens(grp)
        nc.sync.dma_start(out=bo_all[:], in_=bo.partition_broadcast(P))

        ident = keep.tile([P, P], F32)
        make_identity(nc, ident[:])
        same_pos = keep.tile([P, GROUP_POS], F32)
        nc.vector.tensor_reduce(
            out=same_pos[:], in_=ident[:].rearrange("p (s i) -> p s i", i=VIEWS), axis=INNERMOST, op=ADD
        )
        block_mask = keep.tile([P, GROUP_POS, VIEWS], F32)
        nc.vector.tensor_copy(
            out=block_mask[:], in_=same_pos[:].unsqueeze(2).to_broadcast([P, GROUP_POS, VIEWS])
        )

        grouped_weights = {}

        def regroup_weights(name, raw, g):
            for half, copy in enumerate((nc.vector.tensor_copy, nc.scalar.copy)):
                grouped_w = w_stage.tile([P, N_TILE, PACK], BF16, align_bytes=64)
                copy(
                    out=grouped_w[:].rearrange("p (c i) t -> p c t i", i=4),
                    in_=raw[:, g, :, half_cols(half)].rearrange("p t (c i) -> p c t i", i=4),
                )
                grouped_weights[(name, g, half)] = grouped_w

        def quantise_weights(name, codes, scales, g):
            for half in range(N_HALVES):
                nc.vector.quantize_mx(
                    out=codes[:, g, half_cols(half)].bitcast(FP8X4),
                    scales=scales[:, g, half_cols(half)],
                    in_=grouped_weights[(name, g, half)][:].rearrange("p n t -> p (n t)"),
                )

        grouped_tokens = {}

        def transpose_tokens(chunk):
            grouped_x = x_stage.tile([P, SCENES, PASSES, P, PACK], BF16, align_bytes=64)
            for b in range(SCENES):
                words = x_raw[:, chunk * SCENES + b, :].bitcast(F32)
                flipped = psum.tile([P, PACK, P], F32, tag="flip")
                for c in range(PACK):
                    nc.tensor.transpose(flipped[:, c, :], words[:, c * P : (c + 1) * P], ident[:])
                nc.scalar.copy(
                    out=grouped_x[:, b].bitcast(F32), in_=flipped[:].rearrange("p (g u) n -> p g n u", u=2)
                )
            grouped_tokens[chunk] = grouped_x

        def quantise_tokens(chunk):
            groups = slice(chunk * SCENES, (chunk + 1) * SCENES)
            nc.vector.quantize_mx(
                out=x_codes[:, groups, :].rearrange("p b w -> p (b w)").bitcast(FP8X4),
                scales=x_scales[:, groups, :].rearrange("p b w -> p (b w)"),
                in_=grouped_tokens[chunk][:].rearrange("p b g n t -> p (b g n t)"),
            )

        def chunk_that_starts_at(grp):
            chunk, offset = divmod(grp, SCENES)
            return chunk if offset == 0 and 0 <= chunk < CHUNKS else None

        weights_t = keep.tile([P, CHUNKS, SCENES, HEADS, VIEWS], F32)
        piece_shape = [P, PIECE_POS, VIEWS]
        exponents = {}
        piece_weights = {}

        def softmax_shift(piece):
            by_pos = score_raw[:, :, piece * PIECE_POS : (piece + 1) * PIECE_POS].rearrange("p j s -> p s j")
            top = s_pool.tile([P, PIECE_POS], F32)
            nc.vector.tensor_reduce(out=top[:], in_=by_pos, axis=INNERMOST, op=MAX)
            expd = s_pool.tile(piece_shape, F32)
            nc.vector.tensor_tensor(
                out=expd[:], in0=by_pos, in1=top[:].unsqueeze(2).to_broadcast(piece_shape), op=SUBTRACT
            )
            exponents[piece] = expd

        def softmax_exp(piece):
            nc.scalar.activation(out=exponents[piece][:], in_=exponents[piece][:], func=EXP)

        def softmax_normalise(piece):
            total = s_pool.tile([P, PIECE_POS], F32)
            nc.vector.tensor_reduce(out=total[:], in_=exponents[piece][:], axis=INNERMOST, op=ADD)
            inverse = s_pool.tile([P, PIECE_POS], F32)
            nc.vector.reciprocal(out=inverse[:], in_=total[:])
            weights = s_pool.tile([P, PIECE_CHUNKS, P], F32)
            nc.vector.tensor_tensor(
                out=weights[:].rearrange("p c (s j) -> p (c s) j", j=VIEWS),
                in0=exponents[piece][:],
                in1=inverse[:].unsqueeze(2).to_broadcast(piece_shape),
                op=MULT,
            )
            piece_weights[piece] = weights

        def softmax_transpose(piece):
            flipped = psum.tile([P, PACK, P], F32, tag="flip")
            for c in range(PIECE_CHUNKS):
                nc.tensor.transpose(flipped[:, c, :], piece_weights[piece][:, c, :], ident[:])
            chunks = slice(piece * PIECE_CHUNKS, (piece + 1) * PIECE_CHUNKS)
            nc.scalar.copy(
                out=weights_t[:, chunks].rearrange("p c b h i -> p (c b) h i"),
                in_=flipped[:, 0:PIECE_CHUNKS, :].rearrange("p c (b i h) -> p (c b) h i", b=SCENES, i=VIEWS),
            )

        def piece_that_starts_at(grp):
            piece, offset = divmod(grp, PIECE_GROUPS)
            return piece if offset == 0 and 0 <= piece < PIECES else None

        bv_cols = keep.tile([P, HEADS], F32)

        def bias_columns():
            bv_wide = keep.tile([P, P], F32)
            nc.vector.tensor_copy(out=bv_wide[:], in_=bv_rows[:])
            flipped = psum.tile([P, PACK, P], F32, tag="flip")
            nc.tensor.transpose(flipped[:, 0, :], bv_wide[:], ident[:])
            nc.vector.tensor_copy(out=bv_cols[:], in_=flipped[:, 0, 0:HEADS])

        values = {}
        mix_weights = {}
        mix_sums = {}
        mixed_tokens = {}
        mixed_codes = {}
        out_sums = {}

        def first_projection(grp):
            v_rows = v_pool.tile([P, FEATURES], F32)
            for half in range(N_HALVES):
                acc = psum.tile([P, N_TILE], F32, tag="acc_v")
                for g in range(PASSES):
                    toks = slice(g * P, (g + 1) * P)
                    nc.tensor.matmul_mx(
                        out=acc[:],
                        lhsT=x_codes[:, grp, toks].bitcast(FP8X4),
                        lhsT_scale=x_scales[:, grp, toks],
                        rhs=wv_codes[:, g, half_cols(half)].bitcast(FP8X4),
                        rhs_scale=wv_scales[:, g, half_cols(half)],
                        start=(g == 0),
                        stop=(g == PASSES - 1),
                    )
                nc.scalar.copy(out=v_rows[:, half_cols(half)], in_=acc[:])
            values[grp] = v_rows

        def build_mix_weights(grp):
            c, b = chunk_and_scene(grp)
            shape = [P, PACK, GROUP_POS, VIEWS]
            mixw = mixw_pool.tile([P, HEADS, GROUP_POS, VIEWS], F32)
            for g in range(PASSES):
                heads = slice(g * PACK, (g + 1) * PACK)
                nc.gpsimd.tensor_tensor(
                    out=mixw[:, heads],
                    in0=weights_t[:, c, b, heads, :].unsqueeze(2).to_broadcast(shape),
                    in1=block_mask[:].unsqueeze(1).to_broadcast(shape),
                    op=MULT,
                )
            mix_weights[grp] = mixw

        def mix(grp):
            sums = []
            for g in range(PASSES):
                acc = psum.tile([P, PACK, P], F32, tag="acc_mix")
                for t in range(PACK):
                    h = g * PACK + t
                    nc.tensor.matmul(
                        out=acc[:, t, :],
                        lhsT=values[grp][:, h * P : (h + 1) * P],
                        rhs=mix_weights[grp][:, h, :, :].rearrange("p s i -> p (s i)"),
                        start=True,
                        stop=True,
                    )
                sums.append(acc)
            mix_sums[grp] = sums

        def round_mixed(grp):
            mixed = m_pool.tile([P, PASSES, P, PACK], BF16, align_bytes=64)
            for g in range(PASSES):
                nc.vector.tensor_tensor(
                    out=mixed[:, g, :, :],
                    in0=mix_sums[grp][g][:].rearrange("p t n -> p n t"),
                    in1=bv_cols[:, g * PACK : (g + 1) * PACK].unsqueeze(1).to_broadcast([P, P, PACK]),
                    op=ADD,
                )
            mixed_tokens[grp] = mixed

        def quantise_mixed(grp):
            m_codes = m_pool.tile([P, PASSES * P], U32, align_bytes=64)
            m_scales = m_pool.tile([P, PASSES * P], U8, align_bytes=64)
            nc.vector.quantize_mx(
                out=m_codes[:].bitcast(FP8X4),
                scales=m_scales[:],
                in_=mixed_tokens[grp][:].rearrange("p g n t -> p (g n t)"),
            )
            mixed_codes[grp] = (m_codes, m_scales)

        def second_projection(grp):
            m_codes, m_scales = mixed_codes[grp]
            sums = []
            for half in range(N_HALVES):
                acc = psum.tile([P, N_TILE], F32, tag="acc_y")
                for g in range(PASSES):
                    toks = slice(g * P, (g + 1) * P)
                    nc.tensor.matmul_mx(
                        out=acc[:],
                        lhsT=m_codes[:, toks].bitcast(FP8X4),
                        lhsT_scale=m_scales[:, toks],
                        rhs=wo_codes[:, g, half_cols(half)].bitcast(FP8X4),
                        rhs_scale=wo_scales[:, g, half_cols(half)],
                        start=(g == 0),
                        stop=(g == PASSES - 1),
                    )
                sums.append(acc)
            out_sums[grp] = sums

        def finish(grp):
            for half in range(N_HALVES):
                result = y_pool.tile([P, N_TILE], F32)
                nc.vector.tensor_tensor(
                    out=result[:], in0=out_sums[grp][half][:], in1=bo_all[:, half_cols(half)], op=ADD
                )
                nc.sync.dma_start(out=group_rows(out, grp, half_cols(half)), in_=result[:])

        def is_group(grp):
            return 0 <= grp < GROUPS

        def is_pass(g):
            return 0 <= g < PASSES

        wv_start = -(AHEAD_V + AHEAD_X)
        wo_start = BEHIND_Y - PASSES - 1
        for step in range(FIRST_STEP, GROUPS + BEHIND_Y):
            if is_group(step - 1):
                round_mixed(step - 1)
            if is_group(step - BEHIND_Y):
                second_projection(step - BEHIND_Y)
                finish(step - BEHIND_Y)
            if is_group(step - 1):
                quantise_mixed(step - 1)
            if is_pass(step - wv_start - 1):
                quantise_weights("wv", wv_codes, wv_scales, step - wv_start - 1)
            if is_pass(step - wo_start - 1):
                quantise_weights("wo", wo_codes, wo_scales, step - wo_start - 1)
            if is_group(step + AHEAD_V):
                first_projection(step + AHEAD_V)

            piece = piece_that_starts_at(step + AHEAD_W + 2)
            if piece is not None:
                softmax_exp(piece)
            if is_pass(step - wv_start):
                regroup_weights("wv", wv_raw, step - wv_start)
            if is_pass(step - wo_start):
                regroup_weights("wo", wo_raw, step - wo_start)

            piece = piece_that_starts_at(step + AHEAD_W + 1)
            if piece is not None:
                softmax_transpose(piece)
            chunk = chunk_that_starts_at(step + AHEAD_V + AHEAD_X)
            if chunk is not None:
                transpose_tokens(chunk)
            chunk = chunk_that_starts_at(step + AHEAD_V + AHEAD_X - 1)
            if chunk is not None:
                quantise_tokens(chunk)
            if step == -AHEAD_V:
                bias_columns()

            piece = piece_that_starts_at(step + AHEAD_W + 2)
            if piece is not None:
                softmax_normalise(piece)
            piece = piece_that_starts_at(step + AHEAD_W + 3)
            if piece is not None:
                softmax_shift(piece)

            if is_group(step + AHEAD_W):
                build_mix_weights(step + AHEAD_W)
            if is_group(step):
                mix(step)
